import numpy as np
import ml_dtypes


def mxq(x, axis, fmt="e4m3"):
    dtype, down = {"e4m3": (ml_dtypes.float8_e4m3fn, 7), "e5m2": (ml_dtypes.float8_e5m2, 14)}[fmt]
    v = np.moveaxis(np.asarray(x, np.float32).astype(ml_dtypes.bfloat16).astype(np.float64), axis, -1)
    blocks = v.reshape(v.shape[:-1] + (-1, 32))
    amax = np.abs(blocks).max(-1, keepdims=True)
    byte = np.maximum(np.where(amax > 0, np.frexp(amax)[1] - 1 + 127, 0) - down, 1)
    scale = np.exp2(byte - 127.0)
    codes = (blocks / scale).astype(np.float32).astype(dtype).astype(np.float64)
    return np.moveaxis((codes * scale).reshape(v.shape), -1, axis)


WIDE = False


def mx_kscale(k):
    if not WIDE:
        return np.ones(k)
    levels = np.array([10, -10, 5, -5, 0])
    a = np.random.permutation(np.resize(levels, k // 512 * 4)).reshape(k // 512, 4)
    idx = np.arange(k)
    return np.exp2(a[idx // 512, idx % 128 // 32])


BF16 = ml_dtypes.bfloat16


def bf(x):
    return np.asarray(x, np.float32).astype(BF16)


def f64(x):
    return np.asarray(x).astype(np.float64)


B, N, D, F, M1, M2 = 4, 128, 512, 2048, 3, 5
EPS = 1e-12


def erf(z):
    a = np.clip(z, -6.0, 6.0)
    a2 = 2.0 * a * a
    term = a.copy()
    tot = a.copy()
    for k in range(1, 120):
        term = term * (a2 / (2 * k + 1))
        tot = tot + term
    return 2.0 / np.sqrt(np.pi) * np.exp(-a * a) * tot


def gelu(v):
    return 0.5 * v * (1.0 + erf(v / np.sqrt(2.0)))


def setup_inputs():
    s = mx_kscale(D)
    return {'x': bf(np.random.standard_normal((B, N, D, M1)) * s[:, None]),
            'w_in': bf(np.random.standard_normal((D, F)) / np.sqrt(D) / s[:, None]),
            'scale': bf(1.0 + 0.1 * np.random.standard_normal((1, 1, F))),
            'bias': bf(0.3 * np.random.standard_normal((1, 1, F))),
            'w_out': bf(np.random.standard_normal((F, D)) / np.sqrt(F))}


def reference(x, w_in, scale, bias, w_out):
    xq = mxq(f64(x), 2, 'e4m3')
    h = np.swapaxes(np.swapaxes(xq, -1, -2) @ mxq(f64(w_in), 0, 'e4m3'), -1, -2)
    norm = np.maximum(np.sqrt(np.sum(h * h, axis=-1, keepdims=True)), EPS)
    phase = h / norm
    gated = gelu(norm[..., 0] * f64(scale) + f64(bias))[..., None]
    g = gated * phase
    y = np.swapaxes(mxq(g, 2, 'e4m3'), -1, -2) @ mxq(f64(w_out), 0, 'e4m3')
    return np.swapaxes(y, -1, -2)

@@ -1,0 +1,271 @@
+from contextlib import ExitStack
+
+import concourse.mybir as mybir
+from concourse.masks import make_identity
+
+F32 = mybir.dt.float32
+BF16 = mybir.dt.bfloat16
+U32 = mybir.dt.uint32
+U8 = mybir.dt.uint8
+FP8X4 = mybir.dt.float8_e4m3fn_x4
+ACT = mybir.ActivationFunctionType
+ALU = mybir.AluOpType
+
+P = 128
+PACK = 4
+K_PASS = P * PACK
+TOKEN_TILES = 4
+COMPONENTS = 3
+D = 512
+F = 2048
+GROUPS = F // K_PASS
+F_TILES = F // P
+D_PIECES = D // P
+UNITS = TOKEN_TILES * GROUPS
+H_BANKS = 6
+MAX_INVERSE_NORM = 1e12
+FLOPS = 2 * 2 * TOKEN_TILES * P * COMPONENTS * D * F
+
+
+def tile_feedforwardse3_pa_kernel(tc, x, w_in, scale, bias, w_out, out):
+    nc = tc.nc
+    x_rows = x.rearrange("b n d m -> b n (d m)")
+    out_rows = out.rearrange("b n d m -> b n (d m)")
+    w_in_pieces = w_in.rearrange("(j p) (g f) -> g p j f", p=P, g=GROUPS)
+    w_out_pieces = w_out.rearrange("(g j p) d -> g p j d", j=PACK, p=P)
+
+    with ExitStack() as ctx:
+        keep = ctx.enter_context(tc.tile_pool(name="keep", bufs=1))
+        stage = ctx.enter_context(tc.tile_pool(name="stage", bufs=2))
+        psum = ctx.enter_context(tc.psum_pool(name="psum", bufs=1))
+        ctx.enter_context(tc.manual_schedule())
+
+        identity = keep.tile([P, P], BF16)
+        vector_rows = keep.tile([P, P], BF16)
+        one = keep.tile([P, 1], F32)
+        nc.vector.memset(vector_rows[:], 0.0)
+        nc.vector.memset(one[:], 1.0)
+        x_raw = {}
+        w_in_raw = {}
+        w_out_raw = {}
+
+        def load_x(tt):
+            x_raw[tt] = keep.tile([P, D * COMPONENTS], BF16, name="x_raw%d" % tt)
+            nc.sync.dma_start(out=x_raw[tt][:], in_=x_rows[tt])
+
+        def load_weight(raw, pieces, g, name):
+            raw[g] = keep.tile([P, PACK, K_PASS], BF16, name="%s%d" % (name, g))
+            nc.sync.dma_start(out=raw[g][:], in_=pieces[g])
+
+        load_x(0)
+        load_weight(w_in_raw, w_in_pieces, 0, "w_in_raw")
+        nc.sync.dma_start(out=vector_rows[0:F_TILES, :], in_=scale.rearrange("a b (r c) -> (a b r) c", c=P))
+        nc.sync.dma_start(out=vector_rows[F_TILES : 2 * F_TILES, :], in_=bias.rearrange("a b (r c) -> (a b r) c", c=P))
+        for g in range(1, GROUPS):
+            load_weight(w_in_raw, w_in_pieces, g, "w_in_raw")
+        for tt in range(1, TOKEN_TILES):
+            load_x(tt)
+        for g in range(GROUPS):
+            load_weight(w_out_raw, w_out_pieces, g, "w_out_raw")
+
+        make_identity(nc, identity[:])
+        one_out = keep.tile([P, 1], F32)
+        nc.scalar.activation(out=one_out[:], in_=one[:], func=ACT.Abs_reciprocal_sqrt)
+
+        w_grouped = {}
+        w_in_codes = {}
+        w_in_scales = {}
+        w_out_codes = {}
+        w_out_scales = {}
+
+        def regroup_weight(raw, name, g):
+            w_grouped[name, g] = stage.tile([P, K_PASS, PACK], BF16, align_bytes=64, name="w_grouped")
+            nc.vector.tensor_copy(
+                out=w_grouped[name, g][:].rearrange("p (c i) j -> p c j i", i=4),
+                in_=raw[g][:].rearrange("p j (c i) -> p c j i", i=4),
+            )
+
+        def quantise_weight(codes, scales, name, g):
+            codes[g] = keep.tile([P, K_PASS], U32, align_bytes=64, name="%s_codes%d" % (name, g))
+            scales[g] = keep.tile([P, K_PASS], U8, align_bytes=64, name="%s_scales%d" % (name, g))
+            nc.vector.quantize_mx(
+                out=codes[g][:].bitcast(FP8X4), scales=scales[g][:], in_=w_grouped[name, g][:].rearrange("p w j -> p (w j)")
+            )
+
+        x_grouped = {}
+        x_codes = {}
+        x_scales = {}
+        component_runs = ((0, 2), (2, 1))
+
+        def transpose_x(tt):
+            x_dm = x_raw[tt][:].rearrange("p (d m) -> p d m", m=COMPONENTS)
+            x_grouped[tt] = stage.tile([P, COMPONENTS, P, PACK], BF16, align_bytes=64, name="x_grouped")
+            for first, count in component_runs:
+                x_t = psum.tile([P, 2, PACK, P], BF16, tag="acc", bufs=2)
+                for q in range(count):
+                    for c in range(PACK):
+                        nc.tensor.transpose(x_t[:, q, c, :], x_dm[:, c * P : (c + 1) * P, first + q], identity[:])
+                nc.scalar.copy(
+                    out=x_grouped[tt][:, first : first + count],
+                    in_=x_t[:, 0:count].rearrange("p q c t -> p q t c"),
+                )
+
+        def quantise_x(tt):
+            x_codes[tt] = keep.tile([P, COMPONENTS, P], U32, align_bytes=64, name="x_codes%d" % tt)
+            x_scales[tt] = keep.tile([P, COMPONENTS, P], U8, align_bytes=64, name="x_scales%d" % tt)
+            for first, count in component_runs:
+                nc.vector.quantize_mx(
+                    out=x_codes[tt][:, first : first + count, :].rearrange("p q t -> p (q t)").bitcast(FP8X4),
+                    scales=x_scales[tt][:, first : first + count, :].rearrange("p q t -> p (q t)"),
+                    in_=x_grouped[tt][:, first : first + count].rearrange("p q t c -> p (q t c)"),
+                )
+
+        def hidden(tt, g, m):
+            h = psum.tile([P, PACK, P], F32, bufs=H_BANKS)
+            for j in range(PACK):
+                cols = slice(j * P, (j + 1) * P)
+                nc.tensor.matmul_mx(
+                    out=h[:, j, :],
+                    lhsT=w_in_codes[g][:, cols].bitcast(FP8X4),
+                    lhsT_scale=w_in_scales[g][:, cols],
+                    rhs=x_codes[tt][:, m, :].bitcast(FP8X4),
+                    rhs_scale=x_scales[tt][:, m, :],
+                    start=True,
+                    stop=True,
+                )
+            return h
+
+        sum_squares = {}
+        inverse_norm = {}
+        norm = {}
+        gelu = {}
+        g_codes = {}
+        g_scales = {}
+
+        def add_squares(tt, g):
+            square = []
+            for m in range(COMPONENTS):
+                h = hidden(tt, g, m)
+                square.append(stage.tile([P, PACK, P], F32, name="square%d" % m, bufs=2))
+                nc.scalar.activation(out=square[m][:], in_=h[:], func=ACT.Square)
+            two_squares = stage.tile([P, PACK, P], F32)
+            nc.vector.tensor_tensor(out=two_squares[:], in0=square[0][:], in1=square[1][:], op=ALU.add)
+            sum_squares[tt, g] = stage.tile([P, PACK, P], F32, name="sum_squares", bufs=2)
+            nc.vector.tensor_tensor(out=sum_squares[tt, g][:], in0=two_squares[:], in1=square[2][:], op=ALU.add)
+
+        def take_norm(tt, g):
+            inverse_norm[tt, g] = stage.tile([P, PACK, P], F32, name="inverse_norm", bufs=UNITS)
+            nc.scalar.activation(out=inverse_norm[tt, g][:], in_=sum_squares[tt, g][:], func=ACT.Abs_reciprocal_sqrt)
+            norm[tt, g] = stage.tile([P, PACK, P], F32, name="norm", bufs=UNITS)
+            nc.vector.scalar_tensor_tensor(
+                out=norm[tt, g][:],
+                in0=inverse_norm[tt, g][:],
+                scalar=MAX_INVERSE_NORM,
+                in1=sum_squares[tt, g][:],
+                op0=ALU.min,
+                op1=ALU.mult,
+            )
+
+        def take_gelu(tt, g):
+            gelu[tt, g] = stage.tile([P, PACK, P], F32, name="gelu", bufs=3)
+            for j in range(PACK):
+                ft = g * PACK + j
+                nc.scalar.activation(
+                    out=gelu[tt, g][:, j, :],
+                    in_=norm[tt, g][:, j, :],
+                    func=ACT.Gelu,
+                    bias=gain_bias[:, F_TILES + ft : F_TILES + ft + 1],
+                    scale=gain_bias[:, ft : ft + 1],
+                )
+
+        def multiply_by_gate(tt, g):
+            if g == 0:
+                g_codes[tt] = stage.tile([P, GROUPS, COMPONENTS, P], U32, align_bytes=64, name="g_codes")
+                g_scales[tt] = stage.tile([P, GROUPS, COMPONENTS, P], U8, align_bytes=64, name="g_scales")
+            gate = stage.tile([P, P, PACK], F32)
+            nc.vector.scalar_tensor_tensor(
+                out=gate[:],
+                in0=inverse_norm[tt, g][:].rearrange("p j t -> p t j"),
+                scalar=MAX_INVERSE_NORM,
+                in1=gelu[tt, g][:].rearrange("p j t -> p t j"),
+                op0=ALU.min,
+                op1=ALU.mult,
+            )
+            g_grouped = []
+            for m in range(COMPONENTS + 1):
+                if m < COMPONENTS:
+                    h = hidden(tt, g, m)
+                    g_grouped.append(stage.tile([P, P, PACK], BF16, align_bytes=64, name="g_grouped", bufs=3))
+                    nc.vector.tensor_tensor(
+                        out=g_grouped[m][:], in0=h[:].rearrange("p j t -> p t j"), in1=gate[:], op=ALU.mult
+                    )
+                if m >= 1:
+                    nc.vector.quantize_mx(
+                        out=g_codes[tt][:, g, m - 1, :].bitcast(FP8X4),
+                        scales=g_scales[tt][:, g, m - 1, :],
+                        in_=g_grouped[m - 1][:].rearrange("p t j -> p (t j)"),
+                    )
+
+        def second_matmul(tt, piece):
+            acc = psum.tile([P, COMPONENTS, P], F32, tag="acc", bufs=2)
+            cols = slice(piece * P, (piece + 1) * P)
+            for m in range(COMPONENTS):
+                for g in range(GROUPS):
+                    nc.tensor.matmul_mx(
+                        out=acc[:, m, :],
+                        lhsT=g_codes[tt][:, g, m, :].bitcast(FP8X4),
+                        lhsT_scale=g_scales[tt][:, g, m, :],
+                        rhs=w_out_codes[g][:, cols].bitcast(FP8X4),
+                        rhs_scale=w_out_scales[g][:, cols],
+                        start=(g == 0),
+                        stop=(g == GROUPS - 1),
+                    )
+            out_piece = stage.tile([P, P, COMPONENTS], F32, bufs=4)
+            nc.scalar.copy(out=out_piece[:], in_=acc[:].rearrange("p m d -> p d m"))
+            nc.sync.dma_start(
+                out=out_rows[tt][:, piece * P * COMPONENTS : (piece + 1) * P * COMPONENTS],
+                in_=out_piece[:].rearrange("p d m -> p (d m)"),
+            )
+
+        transpose_x(0)
+        vector_cols = psum.tile([P, P], BF16, tag="acc", bufs=2)
+        nc.tensor.transpose(vector_cols[:], vector_rows[:], identity[:])
+        regroup_weight(w_in_raw, "w_in", 0)
+        for g in range(GROUPS):
+            if g + 1 < GROUPS:
+                regroup_weight(w_in_raw, "w_in", g + 1)
+            quantise_weight(w_in_codes, w_in_scales, "w_in", g)
+            if g == 0:
+                quantise_x(0)
+        gain_bias = keep.tile([P, 2 * F_TILES], F32)
+        nc.vector.tensor_copy(out=gain_bias[:], in_=vector_cols[:, 0 : 2 * F_TILES])
+
+        units = [(tt, g) for tt in range(TOKEN_TILES) for g in range(GROUPS)]
+
+        for u in range(UNITS + 1):
+            if u < UNITS:
+                tt, g = units[u]
+                add_squares(tt, g)
+                if g == 0 and tt + 1 < TOKEN_TILES:
+                    transpose_x(tt + 1)
+            if u >= 1:
+                take_norm(*units[u - 1])
+            if u < UNITS:
+                if g == 1 and tt + 1 < TOKEN_TILES:
+                    quantise_x(tt + 1)
+                if tt == 1:
+                    regroup_weight(w_out_raw, "w_out", g)
+                    if g >= 1:
+                        quantise_weight(w_out_codes, w_out_scales, "w_out", g - 1)
+        quantise_weight(w_out_codes, w_out_scales, "w_out", GROUPS - 1)
+
+        take_gelu(*units[0])
+        for u in range(UNITS):
+            tt, g = units[u]
+            if u + 1 < UNITS:
+                take_gelu(*units[u + 1])
+            multiply_by_gate(tt, g)
+            if tt >= 1:
+                second_matmul(tt - 1, g)
+        for piece in range(D_PIECES):
+            second_matmul(TOKEN_TILES - 1, piece)

@@ -191,20 +191,24 @@ def tile_feedforwardse3_pa_kernel(tc, x, w_in, scale, bias, w_out, out):
                 op0=ALU.min,
                 op1=ALU.mult,
             )
-            g_grouped = []
-            for m in range(COMPONENTS + 1):
-                if m < COMPONENTS:
-                    h = hidden(tt, g, m)
-                    g_grouped.append(stage.tile([P, P, PACK], BF16, align_bytes=64, name="g_grouped", bufs=3))
-                    nc.vector.tensor_tensor(
-                        out=g_grouped[m][:], in0=h[:].rearrange("p j t -> p t j"), in1=gate[:], op=ALU.mult
-                    )
-                if m >= 1:
-                    nc.vector.quantize_mx(
-                        out=g_codes[tt][:, g, m - 1, :].bitcast(FP8X4),
-                        scales=g_scales[tt][:, g, m - 1, :],
-                        in_=g_grouped[m - 1][:].rearrange("p t j -> p (t j)"),
-                    )
+            g_grouped = [
+                stage.tile([P, P, PACK], BF16, align_bytes=64, name="g_grouped%d" % m) for m in range(COMPONENTS)
+            ]
+            h = hidden(tt, g, COMPONENTS - 1)
+            h_copy = stage.tile([P, P, PACK], F32)
+            nc.scalar.copy(out=h_copy[:], in_=h[:].rearrange("p j t -> p t j"))
+            nc.gpsimd.tensor_tensor(out=g_grouped[COMPONENTS - 1][:], in0=h_copy[:], in1=gate[:], op=ALU.mult)
+            for m in range(COMPONENTS - 1):
+                h = hidden(tt, g, m)
+                nc.vector.tensor_tensor(
+                    out=g_grouped[m][:], in0=h[:].rearrange("p j t -> p t j"), in1=gate[:], op=ALU.mult
+                )
+            for m in range(COMPONENTS):
+                nc.vector.quantize_mx(
+                    out=g_codes[tt][:, g, m, :].bitcast(FP8X4),
+                    scales=g_scales[tt][:, g, m, :],
+                    in_=g_grouped[m][:].rearrange("p t j -> p (t j)"),
+                )
 
         def second_matmul(tt, piece):
             acc = psum.tile([P, COMPONENTS, P], F32, tag="acc", bufs=2)

@@ -22,7 +22,7 @@ GROUPS = F // K_PASS
 F_TILES = F // P
 D_PIECES = D // P
 UNITS = TOKEN_TILES * GROUPS
-H_BANKS = 6
+BANKS = 8
 MAX_INVERSE_NORM = 1e12
 FLOPS = 2 * 2 * TOKEN_TILES * P * COMPONENTS * D * F
 
@@ -69,6 +69,8 @@ def tile_feedforwardse3_pa_kernel(tc, x, w_in, scale, bias, w_out, out):
             load_weight(w_out_raw, w_out_pieces, g, "w_out_raw")
 
         make_identity(nc, identity[:])
+        identity_f32 = keep.tile([P, P], F32)
+        make_identity(nc, identity_f32[:])
         one_out = keep.tile([P, 1], F32)
         nc.scalar.activation(out=one_out[:], in_=one[:], func=ACT.Abs_reciprocal_sqrt)
 
@@ -101,7 +103,7 @@ def tile_feedforwardse3_pa_kernel(tc, x, w_in, scale, bias, w_out, out):
             x_dm = x_raw[tt][:].rearrange("p (d m) -> p d m", m=COMPONENTS)
             x_grouped[tt] = stage.tile([P, COMPONENTS, P, PACK], BF16, align_bytes=64, name="x_grouped")
             for first, count in component_runs:
-                x_t = psum.tile([P, 2, PACK, P], BF16, tag="acc", bufs=2)
+                x_t = psum.tile([P, 2, PACK, P], BF16, tag="bank", bufs=BANKS)
                 for q in range(count):
                     for c in range(PACK):
                         nc.tensor.transpose(x_t[:, q, c, :], x_dm[:, c * P : (c + 1) * P, first + q], identity[:])
@@ -121,7 +123,7 @@ def tile_feedforwardse3_pa_kernel(tc, x, w_in, scale, bias, w_out, out):
                 )
 
         def hidden(tt, g, m):
-            h = psum.tile([P, PACK, P], F32, bufs=H_BANKS)
+            h = psum.tile([P, PACK, P], F32, tag="bank", bufs=BANKS)
             for j in range(PACK):
                 cols = slice(j * P, (j + 1) * P)
                 nc.tensor.matmul_mx(
@@ -135,6 +137,7 @@ def tile_feedforwardse3_pa_kernel(tc, x, w_in, scale, bias, w_out, out):
                 )
             return h
 
+        squares = {}
         sum_squares = {}
         inverse_norm = {}
         norm = {}
@@ -142,16 +145,34 @@ def tile_feedforwardse3_pa_kernel(tc, x, w_in, scale, bias, w_out, out):
         g_codes = {}
         g_scales = {}
 
-        def add_squares(tt, g):
-            square = []
+        def take_squares(tt, g):
+            squares[tt, g] = []
             for m in range(COMPONENTS):
-                h = hidden(tt, g, m)
-                square.append(stage.tile([P, PACK, P], F32, name="square%d" % m, bufs=2))
-                nc.scalar.activation(out=square[m][:], in_=h[:], func=ACT.Square)
-            two_squares = stage.tile([P, PACK, P], F32)
-            nc.vector.tensor_tensor(out=two_squares[:], in0=square[0][:], in1=square[1][:], op=ALU.add)
-            sum_squares[tt, g] = stage.tile([P, PACK, P], F32, name="sum_squares", bufs=2)
-            nc.vector.tensor_tensor(out=sum_squares[tt, g][:], in0=two_squares[:], in1=square[2][:], op=ALU.add)
+                h = psum.tile([P, K_PASS], F32, tag="bank", bufs=BANKS)
+                nc.tensor.matmul_mx(
+                    out=h[:],
+                    lhsT=x_codes[tt][:, m, :].bitcast(FP8X4),
+                    lhsT_scale=x_scales[tt][:, m, :],
+                    rhs=w_in_codes[g][:].bitcast(FP8X4),
+                    rhs_scale=w_in_scales[g][:],
+                    start=True,
+                    stop=True,
+                )
+                squares[tt, g].append(stage.tile([P, K_PASS], F32, name="square%d" % m, bufs=2))
+                nc.scalar.activation(out=squares[tt, g][m][:], in_=h[:], func=ACT.Square)
+
+        def add_squares(tt, g):
+            sum_squares[tt, g] = psum.tile([P, PACK, P], F32, tag="bank", bufs=BANKS, name="sum_squares")
+            for j in range(PACK):
+                for m in range(COMPONENTS):
+                    nc.tensor.matmul(
+                        sum_squares[tt, g][:, j, :],
+                        lhsT=squares[tt, g][m][:, j * P : (j + 1) * P],
+                        rhs=identity_f32[:],
+                        is_transpose=True,
+                        start=(m == 0),
+                        stop=(m == COMPONENTS - 1),
+                    )
 
         def take_norm(tt, g):
             inverse_norm[tt, g] = stage.tile([P, PACK, P], F32, name="inverse_norm", bufs=UNITS)
@@ -211,7 +232,7 @@ def tile_feedforwardse3_pa_kernel(tc, x, w_in, scale, bias, w_out, out):
                 )
 
         def second_matmul(tt, piece):
-            acc = psum.tile([P, COMPONENTS, P], F32, tag="acc", bufs=2)
+            acc = psum.tile([P, COMPONENTS, P], F32, tag="bank", bufs=BANKS)
             cols = slice(piece * P, (piece + 1) * P)
             for m in range(COMPONENTS):
                 for g in range(GROUPS):
@@ -232,7 +253,7 @@ def tile_feedforwardse3_pa_kernel(tc, x, w_in, scale, bias, w_out, out):
             )
 
         transpose_x(0)
-        vector_cols = psum.tile([P, P], BF16, tag="acc", bufs=2)
+        vector_cols = psum.tile([P, P], BF16, tag="bank", bufs=BANKS)
         nc.tensor.transpose(vector_cols[:], vector_rows[:], identity[:])
         regroup_weight(w_in_raw, "w_in", 0)
         for g in range(GROUPS):
@@ -249,10 +270,11 @@ def tile_feedforwardse3_pa_kernel(tc, x, w_in, scale, bias, w_out, out):
         for u in range(UNITS + 1):
             if u < UNITS:
                 tt, g = units[u]
-                add_squares(tt, g)
+                take_squares(tt, g)
                 if g == 0 and tt + 1 < TOKEN_TILES:
                     transpose_x(tt + 1)
             if u >= 1:
+                add_squares(*units[u - 1])
                 take_norm(*units[u - 1])
             if u < UNITS:
                 if g == 1 and tt + 1 < TOKEN_TILES:

@@ -23,6 +23,7 @@ F_TILES = F // P
 D_PIECES = D // P
 UNITS = TOKEN_TILES * GROUPS
 BANKS = 8
+HIDDEN_BANKS = 5
 MAX_INVERSE_NORM = 1e12
 FLOPS = 2 * 2 * TOKEN_TILES * P * COMPONENTS * D * F
 
@@ -37,7 +38,6 @@ def tile_feedforwardse3_pa_kernel(tc, x, w_in, scale, bias, w_out, out):
     with ExitStack() as ctx:
         keep = ctx.enter_context(tc.tile_pool(name="keep", bufs=1))
         stage = ctx.enter_context(tc.tile_pool(name="stage", bufs=2))
-        psum = ctx.enter_context(tc.psum_pool(name="psum", bufs=1))
         ctx.enter_context(tc.manual_schedule())
 
         identity = keep.tile([P, P], BF16)
@@ -97,33 +97,28 @@ def tile_feedforwardse3_pa_kernel(tc, x, w_in, scale, bias, w_out, out):
         x_grouped = {}
         x_codes = {}
         x_scales = {}
-        component_runs = ((0, 2), (2, 1))
 
-        def transpose_x(tt):
+        def transpose_x(tt, m):
             x_dm = x_raw[tt][:].rearrange("p (d m) -> p d m", m=COMPONENTS)
-            x_grouped[tt] = stage.tile([P, COMPONENTS, P, PACK], BF16, align_bytes=64, name="x_grouped")
-            for first, count in component_runs:
-                x_t = psum.tile([P, 2, PACK, P], BF16, tag="bank", bufs=BANKS)
-                for q in range(count):
-                    for c in range(PACK):
-                        nc.tensor.transpose(x_t[:, q, c, :], x_dm[:, c * P : (c + 1) * P, first + q], identity[:])
-                nc.scalar.copy(
-                    out=x_grouped[tt][:, first : first + count],
-                    in_=x_t[:, 0:count].rearrange("p q c t -> p q t c"),
-                )
+            x_grouped[tt, m] = stage.tile([P, P, PACK], BF16, align_bytes=64, name="x_grouped%d" % m)
+            x_t = psum.tile([P, PACK, P], BF16, tag="hidden" if tt == 0 else "turned", bufs=HIDDEN_BANKS if tt == 0 else 1)
+            for c in range(PACK):
+                nc.tensor.transpose(x_t[:, c, :], x_dm[:, c * P : (c + 1) * P, m], identity[:])
+            copy = nc.scalar.copy if tt == 0 else nc.vector.tensor_copy
+            copy(out=x_grouped[tt, m][:], in_=x_t[:].rearrange("p c t -> p t c"))
 
-        def quantise_x(tt):
-            x_codes[tt] = keep.tile([P, COMPONENTS, P], U32, align_bytes=64, name="x_codes%d" % tt)
-            x_scales[tt] = keep.tile([P, COMPONENTS, P], U8, align_bytes=64, name="x_scales%d" % tt)
-            for first, count in component_runs:
-                nc.vector.quantize_mx(
-                    out=x_codes[tt][:, first : first + count, :].rearrange("p q t -> p (q t)").bitcast(FP8X4),
-                    scales=x_scales[tt][:, first : first + count, :].rearrange("p q t -> p (q t)"),
-                    in_=x_grouped[tt][:, first : first + count].rearrange("p q t c -> p (q t c)"),
-                )
+        def quantise_x(tt, m):
+            if m == 0:
+                x_codes[tt] = keep.tile([P, COMPONENTS, P], U32, align_bytes=64, name="x_codes%d" % tt)
+                x_scales[tt] = keep.tile([P, COMPONENTS, P], U8, align_bytes=64, name="x_scales%d" % tt)
+            nc.vector.quantize_mx(
+                out=x_codes[tt][:, m, :].bitcast(FP8X4),
+                scales=x_scales[tt][:, m, :],
+                in_=x_grouped[tt, m][:].rearrange("p t c -> p (t c)"),
+            )
 
         def hidden(tt, g, m):
-            h = psum.tile([P, PACK, P], F32, tag="bank", bufs=BANKS)
+            h = psum_2.tile([P, PACK, P], F32, tag="bank", bufs=BANKS)
             for j in range(PACK):
                 cols = slice(j * P, (j + 1) * P)
                 nc.tensor.matmul_mx(
@@ -145,10 +140,13 @@ def tile_feedforwardse3_pa_kernel(tc, x, w_in, scale, bias, w_out, out):
         g_codes = {}
         g_scales = {}
 
-        def take_squares(tt, g):
-            squares[tt, g] = []
+        token_hidden = {}
+
+        def hidden_by_token(tt, g):
+            token_hidden[tt, g] = []
             for m in range(COMPONENTS):
-                h = psum.tile([P, K_PASS], F32, tag="bank", bufs=BANKS)
+                h = psum.tile([P, K_PASS], F32, tag="hidden", bufs=HIDDEN_BANKS)
+                token_hidden[tt, g].append(h)
                 nc.tensor.matmul_mx(
                     out=h[:],
                     lhsT=x_codes[tt][:, m, :].bitcast(FP8X4),
@@ -158,11 +156,15 @@ def tile_feedforwardse3_pa_kernel(tc, x, w_in, scale, bias, w_out, out):
                     start=True,
                     stop=True,
                 )
-                squares[tt, g].append(stage.tile([P, K_PASS], F32, name="square%d" % m, bufs=2))
-                nc.scalar.activation(out=squares[tt, g][m][:], in_=h[:], func=ACT.Square)
+
+        def take_squares(tt, g):
+            squares[tt, g] = []
+            for m in range(COMPONENTS):
+                squares[tt, g].append(stage.tile([P, K_PASS], F32, name="square%d" % m, bufs=3))
+                nc.scalar.activation(out=squares[tt, g][m][:], in_=token_hidden[tt, g][m][:], func=ACT.Square)
 
         def add_squares(tt, g):
-            sum_squares[tt, g] = psum.tile([P, PACK, P], F32, tag="bank", bufs=BANKS, name="sum_squares")
+            sum_squares[tt, g] = psum.tile([P, PACK, P], F32, bufs=2, name="sum_squares")
             for j in range(PACK):
                 for m in range(COMPONENTS):
                     nc.tensor.matmul(
@@ -188,7 +190,7 @@ def tile_feedforwardse3_pa_kernel(tc, x, w_in, scale, bias, w_out, out):
             )
 
         def take_gelu(tt, g):
-            gelu[tt, g] = stage.tile([P, PACK, P], F32, name="gelu", bufs=3)
+            gelu[tt, g] = stage.tile([P, PACK, P], F32, name="gelu", bufs=4)
             for j in range(PACK):
                 ft = g * PACK + j
                 nc.scalar.activation(
@@ -199,40 +201,60 @@ def tile_feedforwardse3_pa_kernel(tc, x, w_in, scale, bias, w_out, out):
                     scale=gain_bias[:, ft : ft + 1],
                 )
 
-        def multiply_by_gate(tt, g):
-            if g == 0:
-                g_codes[tt] = stage.tile([P, GROUPS, COMPONENTS, P], U32, align_bytes=64, name="g_codes")
-                g_scales[tt] = stage.tile([P, GROUPS, COMPONENTS, P], U8, align_bytes=64, name="g_scales")
-            gate = stage.tile([P, P, PACK], F32)
+        gate = {}
+        g_grouped = {}
+
+        def take_gate(tt, g):
+            gate[tt, g] = stage.tile([P, P, PACK], F32, name="gate", bufs=3)
             nc.vector.scalar_tensor_tensor(
-                out=gate[:],
+                out=gate[tt, g][:],
                 in0=inverse_norm[tt, g][:].rearrange("p j t -> p t j"),
                 scalar=MAX_INVERSE_NORM,
                 in1=gelu[tt, g][:].rearrange("p j t -> p t j"),
                 op0=ALU.min,
                 op1=ALU.mult,
             )
-            g_grouped = [
-                stage.tile([P, P, PACK], BF16, align_bytes=64, name="g_grouped%d" % m) for m in range(COMPONENTS)
-            ]
-            h = hidden(tt, g, COMPONENTS - 1)
-            h_copy = stage.tile([P, P, PACK], F32)
-            nc.scalar.copy(out=h_copy[:], in_=h[:].rearrange("p j t -> p t j"))
-            nc.gpsimd.tensor_tensor(out=g_grouped[COMPONENTS - 1][:], in0=h_copy[:], in1=gate[:], op=ALU.mult)
-            for m in range(COMPONENTS - 1):
-                h = hidden(tt, g, m)
+
+        channel_hidden = {}
+        h_copy = {}
+
+        def hidden_by_channel(tt, g):
+            for m in (2, 0, 1):
+                channel_hidden[tt, g, m] = hidden(tt, g, m)
+
+        def copy_hidden(tt, g):
+            h_copy[tt, g] = stage.tile([P, P, PACK], F32, name="h_copy")
+            nc.scalar.copy(out=h_copy[tt, g][:], in_=channel_hidden[tt, g, COMPONENTS - 1][:].rearrange("p j t -> p t j"))
+
+        def multiply_by_gate(tt, g, m):
+            g_grouped[tt, g, m] = stage.tile(
+                [P, P, PACK], BF16, align_bytes=64, name="g_grouped%d" % m, bufs=1 if m == COMPONENTS - 1 else 3
+            )
+            if (tt, g, m) in on_gpsimd:
+                nc.gpsimd.tensor_tensor(out=g_grouped[tt, g, m][:], in0=h_copy[tt, g][:], in1=gate[tt, g][:], op=ALU.mult)
+            else:
                 nc.vector.tensor_tensor(
-                    out=g_grouped[m][:], in0=h[:].rearrange("p j t -> p t j"), in1=gate[:], op=ALU.mult
+                    out=g_grouped[tt, g, m][:],
+                    in0=channel_hidden[tt, g, m][:].rearrange("p j t -> p t j"),
+                    in1=gate[tt, g][:],
+                    op=ALU.mult,
                 )
+
+        def quantise_g(tt, g):
+            if g == 0:
+                g_codes[tt] = stage.tile([P, GROUPS, COMPONENTS, P], U32, align_bytes=64, name="g_codes")
+                g_scales[tt] = stage.tile([P, GROUPS, COMPONENTS, P], U8, align_bytes=64, name="g_scales")
             for m in range(COMPONENTS):
                 nc.vector.quantize_mx(
                     out=g_codes[tt][:, g, m, :].bitcast(FP8X4),
                     scales=g_scales[tt][:, g, m, :],
-                    in_=g_grouped[m][:].rearrange("p t j -> p (t j)"),
+                    in_=g_grouped[tt, g, m][:].rearrange("p t j -> p (t j)"),
                 )
 
+        accumulated = {}
+
         def second_matmul(tt, piece):
-            acc = psum.tile([P, COMPONENTS, P], F32, tag="bank", bufs=BANKS)
+            acc = psum_2.tile([P, COMPONENTS, P], F32, tag="bank", bufs=BANKS)
             cols = slice(piece * P, (piece + 1) * P)
             for m in range(COMPONENTS):
                 for g in range(GROUPS):
@@ -245,53 +267,88 @@ def tile_feedforwardse3_pa_kernel(tc, x, w_in, scale, bias, w_out, out):
                         start=(g == 0),
                         stop=(g == GROUPS - 1),
                     )
+            accumulated[tt, piece] = acc
+
+        def store(tt, piece):
             out_piece = stage.tile([P, P, COMPONENTS], F32, bufs=4)
+            acc = accumulated.pop((tt, piece))
             nc.scalar.copy(out=out_piece[:], in_=acc[:].rearrange("p m d -> p d m"))
             nc.sync.dma_start(
                 out=out_rows[tt][:, piece * P * COMPONENTS : (piece + 1) * P * COMPONENTS],
                 in_=out_piece[:].rearrange("p d m -> p (d m)"),
             )
 
-        transpose_x(0)
-        vector_cols = psum.tile([P, P], BF16, tag="bank", bufs=BANKS)
-        nc.tensor.transpose(vector_cols[:], vector_rows[:], identity[:])
-        regroup_weight(w_in_raw, "w_in", 0)
-        for g in range(GROUPS):
-            if g + 1 < GROUPS:
-                regroup_weight(w_in_raw, "w_in", g + 1)
-            quantise_weight(w_in_codes, w_in_scales, "w_in", g)
-            if g == 0:
-                quantise_x(0)
-        gain_bias = keep.tile([P, 2 * F_TILES], F32)
-        nc.vector.tensor_copy(out=gain_bias[:], in_=vector_cols[:, 0 : 2 * F_TILES])
+        with tc.psum_pool(name="psum_1", bufs=1) as psum:
+            for m in range(COMPONENTS):
+                transpose_x(0, m)
+            vector_cols = psum.tile([P, P], BF16, tag="turned")
+            nc.tensor.transpose(vector_cols[:], vector_rows[:], identity[:])
+            regroup_weight(w_in_raw, "w_in", 0)
+            quantise_x(0, 0)
+            quantise_weight(w_in_codes, w_in_scales, "w_in", 0)
+            quantise_x(0, 1)
+            quantise_x(0, 2)
+            gain_bias = keep.tile([P, 2 * F_TILES], F32)
+            regroup_weight(w_in_raw, "w_in", 1)
+            nc.vector.tensor_copy(out=gain_bias[:], in_=vector_cols[:, 0 : 2 * F_TILES])
+            quantise_weight(w_in_codes, w_in_scales, "w_in", 1)
+            regroup_weight(w_in_raw, "w_in", 2)
+            regroup_weight(w_in_raw, "w_in", 3)
+            quantise_weight(w_in_codes, w_in_scales, "w_in", 2)
+            quantise_weight(w_in_codes, w_in_scales, "w_in", 3)
 
-        units = [(tt, g) for tt in range(TOKEN_TILES) for g in range(GROUPS)]
+            units = [(tt, g) for tt in range(TOKEN_TILES) for g in range(GROUPS)]
 
-        for u in range(UNITS + 1):
-            if u < UNITS:
-                tt, g = units[u]
-                take_squares(tt, g)
-                if g == 0 and tt + 1 < TOKEN_TILES:
-                    transpose_x(tt + 1)
-            if u >= 1:
-                add_squares(*units[u - 1])
-                take_norm(*units[u - 1])
-            if u < UNITS:
-                if g == 1 and tt + 1 < TOKEN_TILES:
-                    quantise_x(tt + 1)
-                if tt == 1:
+            hidden_by_token(*units[0])
+            for u in range(UNITS + 2):
+                tt, g = units[min(u, UNITS - 1)]
+                next_tile = tt + 1 if u < UNITS and tt + 1 < TOKEN_TILES else None
+                if next_tile is not None and g >= 1:
+                    quantise_x(next_tile, g - 1)
+                if u + 1 < UNITS:
+                    hidden_by_token(*units[u + 1])
+                if u < UNITS:
+                    take_squares(tt, g)
+                if next_tile is not None and g < COMPONENTS:
+                    transpose_x(next_tile, g)
+                if 1 <= u <= UNITS:
+                    add_squares(*units[u - 1])
+                if u < UNITS and tt == 1:
                     regroup_weight(w_out_raw, "w_out", g)
                     if g >= 1:
                         quantise_weight(w_out_codes, w_out_scales, "w_out", g - 1)
-        quantise_weight(w_out_codes, w_out_scales, "w_out", GROUPS - 1)
+                if u >= 2:
+                    take_norm(*units[u - 2])
+            quantise_weight(w_out_codes, w_out_scales, "w_out", GROUPS - 1)
 
-        take_gelu(*units[0])
-        for u in range(UNITS):
-            tt, g = units[u]
-            if u + 1 < UNITS:
-                take_gelu(*units[u + 1])
-            multiply_by_gate(tt, g)
-            if tt >= 1:
-                second_matmul(tt - 1, g)
-        for piece in range(D_PIECES):
-            second_matmul(TOKEN_TILES - 1, piece)
+        with tc.psum_pool(name="psum_2", bufs=1) as psum_2:
+            on_gpsimd = [(tt, g, COMPONENTS - 1) for tt, g in units[: UNITS - 1]]
+            pieces = [(tt, piece) for tt in range(TOKEN_TILES) for piece in range(D_PIECES)]
+            take_gelu(*units[0])
+            hidden_by_channel(*units[0])
+            take_gelu(*units[1])
+            take_gate(*units[0])
+            for u in range(UNITS):
+                if u + 1 < UNITS:
+                    hidden_by_channel(*units[u + 1])
+                    copy_hidden(*units[u])
+                if u >= 1:
+                    multiply_by_gate(*units[u - 1], COMPONENTS - 1)
+                for m in range(COMPONENTS - 1):
+                    multiply_by_gate(*units[u], m)
+                if u + 2 < UNITS:
+                    take_gelu(*units[u + 2])
+                if u + 1 < UNITS:
+                    take_gate(*units[u + 1])
+                if u >= 1:
+                    quantise_g(*units[u - 1])
+                for finished in list(accumulated):
+                    store(*finished)
+                if u > GROUPS:
+                    second_matmul(*pieces[u - GROUPS - 1])
+            multiply_by_gate(*units[UNITS - 1], COMPONENTS - 1)
+            quantise_g(*units[UNITS - 1])
+            for tt, piece in pieces[UNITS - GROUPS - 1 :]:
+                second_matmul(tt, piece)
+                for finished in list(accumulated):
+                    store(*finished)

@@ -216,29 +216,21 @@ def tile_feedforwardse3_pa_kernel(tc, x, w_in, scale, bias, w_out, out):
             )
 
         channel_hidden = {}
-        h_copy = {}
 
         def hidden_by_channel(tt, g):
-            for m in (2, 0, 1):
+            for m in range(COMPONENTS):
                 channel_hidden[tt, g, m] = hidden(tt, g, m)
-
-        def copy_hidden(tt, g):
-            h_copy[tt, g] = stage.tile([P, P, PACK], F32, name="h_copy")
-            nc.scalar.copy(out=h_copy[tt, g][:], in_=channel_hidden[tt, g, COMPONENTS - 1][:].rearrange("p j t -> p t j"))
 
         def multiply_by_gate(tt, g, m):
             g_grouped[tt, g, m] = stage.tile(
-                [P, P, PACK], BF16, align_bytes=64, name="g_grouped%d" % m, bufs=1 if m == COMPONENTS - 1 else 3
+                [P, P, PACK], BF16, align_bytes=64, name="g_grouped%d" % m, bufs=3
             )
-            if (tt, g, m) in on_gpsimd:
-                nc.gpsimd.tensor_tensor(out=g_grouped[tt, g, m][:], in0=h_copy[tt, g][:], in1=gate[tt, g][:], op=ALU.mult)
-            else:
-                nc.vector.tensor_tensor(
-                    out=g_grouped[tt, g, m][:],
-                    in0=channel_hidden[tt, g, m][:].rearrange("p j t -> p t j"),
-                    in1=gate[tt, g][:],
-                    op=ALU.mult,
-                )
+            nc.vector.tensor_tensor(
+                out=g_grouped[tt, g, m][:],
+                in0=channel_hidden[tt, g, m][:].rearrange("p j t -> p t j"),
+                in1=gate[tt, g][:],
+                op=ALU.mult,
+            )
 
         def quantise_g(tt, g):
             if g == 0:
@@ -322,7 +314,6 @@ def tile_feedforwardse3_pa_kernel(tc, x, w_in, scale, bias, w_out, out):
             quantise_weight(w_out_codes, w_out_scales, "w_out", GROUPS - 1)
 
         with tc.psum_pool(name="psum_2", bufs=1) as psum_2:
-            on_gpsimd = [(tt, g, COMPONENTS - 1) for tt, g in units[: UNITS - 1]]
             pieces = [(tt, piece) for tt in range(TOKEN_TILES) for piece in range(D_PIECES)]
             take_gelu(*units[0])
             hidden_by_channel(*units[0])
@@ -331,10 +322,7 @@ def tile_feedforwardse3_pa_kernel(tc, x, w_in, scale, bias, w_out, out):
             for u in range(UNITS):
                 if u + 1 < UNITS:
                     hidden_by_channel(*units[u + 1])
-                    copy_hidden(*units[u])
-                if u >= 1:
-                    multiply_by_gate(*units[u - 1], COMPONENTS - 1)
-                for m in range(COMPONENTS - 1):
+                for m in range(COMPONENTS):
                     multiply_by_gate(*units[u], m)
                 if u + 2 < UNITS:
                     take_gelu(*units[u + 2])
@@ -346,7 +334,6 @@ def tile_feedforwardse3_pa_kernel(tc, x, w_in, scale, bias, w_out, out):
                     store(*finished)
                 if u > GROUPS:
                     second_matmul(*pieces[u - GROUPS - 1])
-            multiply_by_gate(*units[UNITS - 1], COMPONENTS - 1)
             quantise_g(*units[UNITS - 1])
             for tt, piece in pieces[UNITS - GROUPS - 1 :]:
                 second_matmul(tt, piece)

@@ -25,6 +25,8 @@ UNITS = TOKEN_TILES * GROUPS
 BANKS = 8
 HIDDEN_BANKS = 5
 MAX_INVERSE_NORM = 1e12
+GPSIMD_TOKENS = 96
+W_OUT_UNITS = (6, 9, 12)
 FLOPS = 2 * 2 * TOKEN_TILES * P * COMPONENTS * D * F
 
 
@@ -118,7 +120,7 @@ def tile_feedforwardse3_pa_kernel(tc, x, w_in, scale, bias, w_out, out):
             )
 
         def hidden(tt, g, m):
-            h = psum_2.tile([P, PACK, P], F32, tag="bank", bufs=BANKS)
+            h = psum_2.tile([P, PACK, P], F32, tag="hidden", bufs=6)
             for j in range(PACK):
                 cols = slice(j * P, (j + 1) * P)
                 nc.tensor.matmul_mx(
@@ -163,17 +165,29 @@ def tile_feedforwardse3_pa_kernel(tc, x, w_in, scale, bias, w_out, out):
                 squares[tt, g].append(stage.tile([P, K_PASS], F32, name="square%d" % m, bufs=3))
                 nc.scalar.activation(out=squares[tt, g][m][:], in_=token_hidden[tt, g][m][:], func=ACT.Square)
 
+        two_squares = {}
+
+        def add_two_squares(tt, g):
+            two_squares[tt, g] = stage.tile([P, K_PASS], F32, name="two_squares", bufs=3)
+            nc.vector.tensor_tensor(
+                out=two_squares[tt, g][:], in0=squares[tt, g][0][:], in1=squares[tt, g][1][:], op=ALU.add
+            )
+
         def add_squares(tt, g):
-            sum_squares[tt, g] = psum.tile([P, PACK, P], F32, bufs=2, name="sum_squares")
+            if (tt, g) in units[UNITS - 2 :]:
+                sum_squares[tt, g] = psum.tile([P, PACK, P], F32, tag="hidden", bufs=HIDDEN_BANKS, name="last_sums")
+            else:
+                sum_squares[tt, g] = psum.tile([P, PACK, P], F32, bufs=2, name="sum_squares")
+            addends = [two_squares[tt, g], squares[tt, g][2]] if (tt, g) in two_squares else squares[tt, g]
             for j in range(PACK):
-                for m in range(COMPONENTS):
+                for addend in addends:
                     nc.tensor.matmul(
                         sum_squares[tt, g][:, j, :],
-                        lhsT=squares[tt, g][m][:, j * P : (j + 1) * P],
+                        lhsT=addend[:, j * P : (j + 1) * P],
                         rhs=identity_f32[:],
                         is_transpose=True,
-                        start=(m == 0),
-                        stop=(m == COMPONENTS - 1),
+                        start=addend is addends[0],
+                        stop=addend is addends[-1],
                     )
 
         def take_norm(tt, g):
@@ -216,19 +230,31 @@ def tile_feedforwardse3_pa_kernel(tc, x, w_in, scale, bias, w_out, out):
             )
 
         channel_hidden = {}
+        h_copy = {}
 
         def hidden_by_channel(tt, g):
-            for m in range(COMPONENTS):
+            for m in (2, 0, 1):
                 channel_hidden[tt, g, m] = hidden(tt, g, m)
 
-        def multiply_by_gate(tt, g, m):
-            g_grouped[tt, g, m] = stage.tile(
-                [P, P, PACK], BF16, align_bytes=64, name="g_grouped%d" % m, bufs=3
+        def copy_hidden(tt, g):
+            h_copy[tt, g] = stage.tile([P, GPSIMD_TOKENS, PACK], F32, name="h_copy")
+            nc.scalar.copy(
+                out=h_copy[tt, g][:],
+                in_=channel_hidden[tt, g, COMPONENTS - 1][:, :, 0:GPSIMD_TOKENS].rearrange("p j t -> p t j"),
             )
+
+        def multiply_by_gate(tt, g, m):
+            g_grouped[tt, g, m] = stage.tile([P, P, PACK], BF16, align_bytes=64, name="g_grouped%d" % m, bufs=2)
+            first = 0
+            if m == COMPONENTS - 1:
+                first = GPSIMD_TOKENS
+                nc.gpsimd.tensor_tensor(
+                    out=g_grouped[tt, g, m][:, 0:first], in0=h_copy[tt, g][:], in1=gate[tt, g][:, 0:first], op=ALU.mult
+                )
             nc.vector.tensor_tensor(
-                out=g_grouped[tt, g, m][:],
-                in0=channel_hidden[tt, g, m][:].rearrange("p j t -> p t j"),
-                in1=gate[tt, g][:],
+                out=g_grouped[tt, g, m][:, first:],
+                in0=channel_hidden[tt, g, m][:, :, first:].rearrange("p j t -> p t j"),
+                in1=gate[tt, g][:, first:],
                 op=ALU.mult,
             )
 
@@ -245,26 +271,34 @@ def tile_feedforwardse3_pa_kernel(tc, x, w_in, scale, bias, w_out, out):
 
         accumulated = {}
 
-        def second_matmul(tt, piece):
-            acc = psum_2.tile([P, COMPONENTS, P], F32, tag="bank", bufs=BANKS)
+        def second_matmul(tt, piece, groups=range(GROUPS)):
+            if len(groups) < GROUPS:
+                acc = psum_2.tile([P, COMPONENTS, P], F32, tag="hidden", bufs=6)
+            else:
+                acc = psum_2.tile([P, COMPONENTS, P], F32, bufs=2)
             cols = slice(piece * P, (piece + 1) * P)
             for m in range(COMPONENTS):
-                for g in range(GROUPS):
+                for g in groups:
                     nc.tensor.matmul_mx(
                         out=acc[:, m, :],
                         lhsT=g_codes[tt][:, g, m, :].bitcast(FP8X4),
                         lhsT_scale=g_scales[tt][:, g, m, :],
                         rhs=w_out_codes[g][:, cols].bitcast(FP8X4),
                         rhs_scale=w_out_scales[g][:, cols],
-                        start=(g == 0),
-                        stop=(g == GROUPS - 1),
+                        start=(g == groups[0]),
+                        stop=(g == groups[-1]),
                     )
             accumulated[tt, piece] = acc
 
-        def store(tt, piece):
+        def store(tt, piece, partial=None):
             out_piece = stage.tile([P, P, COMPONENTS], F32, bufs=4)
             acc = accumulated.pop((tt, piece))
-            nc.scalar.copy(out=out_piece[:], in_=acc[:].rearrange("p m d -> p d m"))
+            if partial is None:
+                nc.scalar.copy(out=out_piece[:], in_=acc[:].rearrange("p m d -> p d m"))
+            else:
+                nc.vector.tensor_tensor(
+                    out=out_piece[:], in0=acc[:].rearrange("p m d -> p d m"), in1=partial[:], op=ALU.add
+                )
             nc.sync.dma_start(
                 out=out_rows[tt][:, piece * P * COMPONENTS : (piece + 1) * P * COMPONENTS],
                 in_=out_piece[:].rearrange("p d m -> p (d m)"),
@@ -285,9 +319,7 @@ def tile_feedforwardse3_pa_kernel(tc, x, w_in, scale, bias, w_out, out):
             nc.vector.tensor_copy(out=gain_bias[:], in_=vector_cols[:, 0 : 2 * F_TILES])
             quantise_weight(w_in_codes, w_in_scales, "w_in", 1)
             regroup_weight(w_in_raw, "w_in", 2)
-            regroup_weight(w_in_raw, "w_in", 3)
             quantise_weight(w_in_codes, w_in_scales, "w_in", 2)
-            quantise_weight(w_in_codes, w_in_scales, "w_in", 3)
 
             units = [(tt, g) for tt in range(TOKEN_TILES) for g in range(GROUPS)]
 
@@ -295,47 +327,67 @@ def tile_feedforwardse3_pa_kernel(tc, x, w_in, scale, bias, w_out, out):
             for u in range(UNITS + 2):
                 tt, g = units[min(u, UNITS - 1)]
                 next_tile = tt + 1 if u < UNITS and tt + 1 < TOKEN_TILES else None
-                if next_tile is not None and g >= 1:
-                    quantise_x(next_tile, g - 1)
+                if next_tile is not None and g < COMPONENTS:
+                    transpose_x(next_tile, g)
                 if u + 1 < UNITS:
                     hidden_by_token(*units[u + 1])
                 if u < UNITS:
                     take_squares(tt, g)
-                if next_tile is not None and g < COMPONENTS:
-                    transpose_x(next_tile, g)
+                    if u in W_OUT_UNITS:
+                        regroup_weight(w_out_raw, "w_out", W_OUT_UNITS.index(u))
+                    if tt >= 1:
+                        add_two_squares(tt, g)
+                    if next_tile is not None and g < COMPONENTS:
+                        quantise_x(next_tile, g)
                 if 1 <= u <= UNITS:
                     add_squares(*units[u - 1])
-                if u < UNITS and tt == 1:
-                    regroup_weight(w_out_raw, "w_out", g)
-                    if g >= 1:
-                        quantise_weight(w_out_codes, w_out_scales, "w_out", g - 1)
                 if u >= 2:
                     take_norm(*units[u - 2])
+                if u in W_OUT_UNITS:
+                    quantise_weight(w_out_codes, w_out_scales, "w_out", W_OUT_UNITS.index(u))
+                if u == 0:
+                    regroup_weight(w_in_raw, "w_in", 3)
+                    quantise_weight(w_in_codes, w_in_scales, "w_in", 3)
+            regroup_weight(w_out_raw, "w_out", GROUPS - 1)
             quantise_weight(w_out_codes, w_out_scales, "w_out", GROUPS - 1)
 
         with tc.psum_pool(name="psum_2", bufs=1) as psum_2:
             pieces = [(tt, piece) for tt in range(TOKEN_TILES) for piece in range(D_PIECES)]
             take_gelu(*units[0])
             hidden_by_channel(*units[0])
+            copy_hidden(*units[0])
             take_gelu(*units[1])
             take_gate(*units[0])
+            last_tile = TOKEN_TILES - 1
+            pieces_done = 0
             for u in range(UNITS):
+                for finished in list(accumulated):
+                    store(*finished)
                 if u + 1 < UNITS:
                     hidden_by_channel(*units[u + 1])
+                    copy_hidden(*units[u + 1])
+                if u == UNITS - 1:
+                    quantise_g(*units[u - 1])
                 for m in range(COMPONENTS):
                     multiply_by_gate(*units[u], m)
                 if u + 2 < UNITS:
                     take_gelu(*units[u + 2])
                 if u + 1 < UNITS:
                     take_gate(*units[u + 1])
-                if u >= 1:
+                if 1 <= u < UNITS - 1:
                     quantise_g(*units[u - 1])
-                for finished in list(accumulated):
-                    store(*finished)
                 if u > GROUPS:
-                    second_matmul(*pieces[u - GROUPS - 1])
+                    for piece in pieces[pieces_done : pieces_done + (2 if u == UNITS - GROUPS + 1 else 1)]:
+                        second_matmul(*piece)
+                        pieces_done = pieces_done + 1
+            for finished in list(accumulated):
+                store(*finished)
             quantise_g(*units[UNITS - 1])
-            for tt, piece in pieces[UNITS - GROUPS - 1 :]:
-                second_matmul(tt, piece)
-                for finished in list(accumulated):
-                    store(*finished)
+            partial = []
+            for piece in range(D_PIECES):
+                second_matmul(last_tile, piece, range(GROUPS - 1))
+                partial.append(stage.tile([P, P, COMPONENTS], F32, name="partial%d" % piece, bufs=1))
+                nc.scalar.copy(out=partial[piece][:], in_=accumulated.pop((last_tile, piece))[:].rearrange("p m d -> p d m"))
+            for piece in range(D_PIECES):
+                second_matmul(last_tile, piece, range(GROUPS - 1, GROUPS))
+                store(last_tile, piece, partial[piece])

@@ -25,8 +25,15 @@ UNITS = TOKEN_TILES * GROUPS
 BANKS = 8
 HIDDEN_BANKS = 5
 MAX_INVERSE_NORM = 1e12
-GPSIMD_TOKENS = 96
-W_OUT_UNITS = (6, 9, 12)
+RUN = 4
+RUNS = P // RUN
+GPSIMD_RUN = 3
+X_EARLY = ((1, 0), (1, 1), (1, 2))
+X_ON_SCALAR = ((0, 0), (0, 1), (0, 2))
+WALK = [(0, 0), (0, 1), (1, 0), (1, 1), (0, 2), (1, 2), (0, 3), (1, 3), (2, 0), (2, 1), (2, 2), (2, 3), (3, 0), (3, 1), (3, 2), (3, 3)]
+X_JOBS = {0: [(1, 0), (1, 1), (1, 2)], 4: [(2, 0)], 5: [(2, 1)], 6: [(2, 2)], 8: [(3, 0)], 9: [(3, 1)], 10: [(3, 2)]}
+W_JOBS = {1: (2,), 2: (3,), 7: (4,), 11: (5,), 13: (6,)}
+V_ADD = (4, 5, 6, 7, 8, 9, 10, 11, 12, 13, 14, 15)
 FLOPS = 2 * 2 * TOKEN_TILES * P * COMPONENTS * D * F
 
 
@@ -63,9 +70,11 @@ def tile_feedforwardse3_pa_kernel(tc, x, w_in, scale, bias, w_out, out):
         load_weight(w_in_raw, w_in_pieces, 0, "w_in_raw")
         nc.sync.dma_start(out=vector_rows[0:F_TILES, :], in_=scale.rearrange("a b (r c) -> (a b r) c", c=P))
         nc.sync.dma_start(out=vector_rows[F_TILES : 2 * F_TILES, :], in_=bias.rearrange("a b (r c) -> (a b r) c", c=P))
-        for g in range(1, GROUPS):
+        load_weight(w_in_raw, w_in_pieces, 1, "w_in_raw")
+        load_x(1)
+        for g in range(2, GROUPS):
             load_weight(w_in_raw, w_in_pieces, g, "w_in_raw")
-        for tt in range(1, TOKEN_TILES):
+        for tt in range(2, TOKEN_TILES):
             load_x(tt)
         for g in range(GROUPS):
             load_weight(w_out_raw, w_out_pieces, g, "w_out_raw")
@@ -103,11 +112,11 @@ def tile_feedforwardse3_pa_kernel(tc, x, w_in, scale, bias, w_out, out):
         def transpose_x(tt, m):
             x_dm = x_raw[tt][:].rearrange("p (d m) -> p d m", m=COMPONENTS)
             x_grouped[tt, m] = stage.tile([P, P, PACK], BF16, align_bytes=64, name="x_grouped%d" % m)
-            x_t = psum.tile([P, PACK, P], BF16, tag="hidden" if tt == 0 else "turned", bufs=HIDDEN_BANKS if tt == 0 else 1)
+            x_t = psum.tile([P, PACK, P], BF16, tag="hidden" if tt == 0 else "sum_squares" if tt == 1 and m >= 1 and X_EARLY else "turned", bufs=HIDDEN_BANKS if tt == 0 else 2 if tt == 1 and m >= 1 and X_EARLY else 1)
             for c in range(PACK):
                 nc.tensor.transpose(x_t[:, c, :], x_dm[:, c * P : (c + 1) * P, m], identity[:])
-            copy = nc.scalar.copy if tt == 0 else nc.vector.tensor_copy
-            copy(out=x_grouped[tt, m][:], in_=x_t[:].rearrange("p c t -> p t c"))
+            copy = nc.scalar.copy if (tt, m) in X_ON_SCALAR else nc.vector.tensor_copy
+            copy(out=x_grouped[tt, m][:].rearrange("p (c i) j -> p c i j", i=RUN), in_=x_t[:].rearrange("p j (i c) -> p c i j", i=RUN))
 
         def quantise_x(tt, m):
             if m == 0:
@@ -162,8 +171,9 @@ def tile_feedforwardse3_pa_kernel(tc, x, w_in, scale, bias, w_out, out):
         def take_squares(tt, g):
             squares[tt, g] = []
             for m in range(COMPONENTS):
-                squares[tt, g].append(stage.tile([P, K_PASS], F32, name="square%d" % m, bufs=3))
-                nc.scalar.activation(out=squares[tt, g][m][:], in_=token_hidden[tt, g][m][:], func=ACT.Square)
+                square = stage.tile([P, K_PASS], F32, name="square%d" % m, bufs=3)
+                squares[tt, g].append(square)
+                nc.scalar.activation(out=square[:], in_=token_hidden[tt, g][m][:], func=ACT.Square)
 
         two_squares = {}
 
@@ -174,15 +184,15 @@ def tile_feedforwardse3_pa_kernel(tc, x, w_in, scale, bias, w_out, out):
             )
 
         def add_squares(tt, g):
-            if (tt, g) in units[UNITS - 2 :]:
-                sum_squares[tt, g] = psum.tile([P, PACK, P], F32, tag="hidden", bufs=HIDDEN_BANKS, name="last_sums")
+            if (tt, g) in walk[UNITS - 2 :]:
+                sum_squares[tt, g] = psum.tile([P, RUNS, PACK, RUN], F32, tag="hidden", bufs=HIDDEN_BANKS, name="last_sums")
             else:
-                sum_squares[tt, g] = psum.tile([P, PACK, P], F32, bufs=2, name="sum_squares")
+                sum_squares[tt, g] = psum.tile([P, RUNS, PACK, RUN], F32, bufs=2, name="sum_squares")
             addends = [two_squares[tt, g], squares[tt, g][2]] if (tt, g) in two_squares else squares[tt, g]
             for j in range(PACK):
                 for addend in addends:
                     nc.tensor.matmul(
-                        sum_squares[tt, g][:, j, :],
+                        sum_squares[tt, g][:, :, j, :],
                         lhsT=addend[:, j * P : (j + 1) * P],
                         rhs=identity_f32[:],
                         is_transpose=True,
@@ -191,9 +201,9 @@ def tile_feedforwardse3_pa_kernel(tc, x, w_in, scale, bias, w_out, out):
                     )
 
         def take_norm(tt, g):
-            inverse_norm[tt, g] = stage.tile([P, PACK, P], F32, name="inverse_norm", bufs=UNITS)
+            inverse_norm[tt, g] = stage.tile([P, RUNS, PACK, RUN], F32, name="inverse_norm", bufs=UNITS)
             nc.scalar.activation(out=inverse_norm[tt, g][:], in_=sum_squares[tt, g][:], func=ACT.Abs_reciprocal_sqrt)
-            norm[tt, g] = stage.tile([P, PACK, P], F32, name="norm", bufs=UNITS)
+            norm[tt, g] = stage.tile([P, RUNS, PACK, RUN], F32, name="norm", bufs=UNITS)
             nc.vector.scalar_tensor_tensor(
                 out=norm[tt, g][:],
                 in0=inverse_norm[tt, g][:],
@@ -204,12 +214,12 @@ def tile_feedforwardse3_pa_kernel(tc, x, w_in, scale, bias, w_out, out):
             )
 
         def take_gelu(tt, g):
-            gelu[tt, g] = stage.tile([P, PACK, P], F32, name="gelu", bufs=4)
+            gelu[tt, g] = stage.tile([P, RUNS, PACK, RUN], F32, name="gelu", bufs=4)
             for j in range(PACK):
                 ft = g * PACK + j
                 nc.scalar.activation(
-                    out=gelu[tt, g][:, j, :],
-                    in_=norm[tt, g][:, j, :],
+                    out=gelu[tt, g][:, :, j, :],
+                    in_=norm[tt, g][:, :, j, :],
                     func=ACT.Gelu,
                     bias=gain_bias[:, F_TILES + ft : F_TILES + ft + 1],
                     scale=gain_bias[:, ft : ft + 1],
@@ -219,12 +229,12 @@ def tile_feedforwardse3_pa_kernel(tc, x, w_in, scale, bias, w_out, out):
         g_grouped = {}
 
         def take_gate(tt, g):
-            gate[tt, g] = stage.tile([P, P, PACK], F32, name="gate", bufs=3)
+            gate[tt, g] = stage.tile([P, RUN, RUNS, PACK], F32, name="gate", bufs=3)
             nc.vector.scalar_tensor_tensor(
-                out=gate[tt, g][:],
-                in0=inverse_norm[tt, g][:].rearrange("p j t -> p t j"),
+                out=gate[tt, g][:].rearrange("p i c j -> p (c j) i"),
+                in0=inverse_norm[tt, g][:].rearrange("p c j i -> p (c j) i"),
                 scalar=MAX_INVERSE_NORM,
-                in1=gelu[tt, g][:].rearrange("p j t -> p t j"),
+                in1=gelu[tt, g][:].rearrange("p c j i -> p (c j) i"),
                 op0=ALU.min,
                 op1=ALU.mult,
             )
@@ -237,23 +247,23 @@ def tile_feedforwardse3_pa_kernel(tc, x, w_in, scale, bias, w_out, out):
                 channel_hidden[tt, g, m] = hidden(tt, g, m)
 
         def copy_hidden(tt, g):
-            h_copy[tt, g] = stage.tile([P, GPSIMD_TOKENS, PACK], F32, name="h_copy")
+            h_copy[tt, g] = stage.tile([P, GPSIMD_RUN, RUNS, PACK], F32, name="h_copy")
             nc.scalar.copy(
                 out=h_copy[tt, g][:],
-                in_=channel_hidden[tt, g, COMPONENTS - 1][:, :, 0:GPSIMD_TOKENS].rearrange("p j t -> p t j"),
+                in_=channel_hidden[tt, g, COMPONENTS - 1][:].rearrange("p j (c i) -> p i c j", i=RUN)[:, 0:GPSIMD_RUN],
             )
 
         def multiply_by_gate(tt, g, m):
-            g_grouped[tt, g, m] = stage.tile([P, P, PACK], BF16, align_bytes=64, name="g_grouped%d" % m, bufs=2)
+            g_grouped[tt, g, m] = stage.tile([P, RUN, RUNS, PACK], BF16, align_bytes=64, name="g_grouped%d" % m, bufs=2)
             first = 0
             if m == COMPONENTS - 1:
-                first = GPSIMD_TOKENS
+                first = GPSIMD_RUN
                 nc.gpsimd.tensor_tensor(
                     out=g_grouped[tt, g, m][:, 0:first], in0=h_copy[tt, g][:], in1=gate[tt, g][:, 0:first], op=ALU.mult
                 )
             nc.vector.tensor_tensor(
                 out=g_grouped[tt, g, m][:, first:],
-                in0=channel_hidden[tt, g, m][:, :, first:].rearrange("p j t -> p t j"),
+                in0=channel_hidden[tt, g, m][:].rearrange("p j (c i) -> p i c j", i=RUN)[:, first:],
                 in1=gate[tt, g][:, first:],
                 op=ALU.mult,
             )
@@ -266,7 +276,7 @@ def tile_feedforwardse3_pa_kernel(tc, x, w_in, scale, bias, w_out, out):
                 nc.vector.quantize_mx(
                     out=g_codes[tt][:, g, m, :].bitcast(FP8X4),
                     scales=g_scales[tt][:, g, m, :],
-                    in_=g_grouped[tt, g, m][:].rearrange("p t j -> p (t j)"),
+                    in_=g_grouped[tt, g, m][:].rearrange("p i c j -> p (i c j)"),
                 )
 
         accumulated = {}
@@ -318,36 +328,38 @@ def tile_feedforwardse3_pa_kernel(tc, x, w_in, scale, bias, w_out, out):
             regroup_weight(w_in_raw, "w_in", 1)
             nc.vector.tensor_copy(out=gain_bias[:], in_=vector_cols[:, 0 : 2 * F_TILES])
             quantise_weight(w_in_codes, w_in_scales, "w_in", 1)
-            regroup_weight(w_in_raw, "w_in", 2)
-            quantise_weight(w_in_codes, w_in_scales, "w_in", 2)
-
             units = [(tt, g) for tt in range(TOKEN_TILES) for g in range(GROUPS)]
-
-            hidden_by_token(*units[0])
+            walk = WALK
+            hidden_by_token(*walk[0])
+            for tt, m in X_EARLY:
+                transpose_x(tt, m)
             for u in range(UNITS + 2):
-                tt, g = units[min(u, UNITS - 1)]
-                next_tile = tt + 1 if u < UNITS and tt + 1 < TOKEN_TILES else None
-                if next_tile is not None and g < COMPONENTS:
-                    transpose_x(next_tile, g)
                 if u + 1 < UNITS:
-                    hidden_by_token(*units[u + 1])
+                    hidden_by_token(*walk[u + 1])
+                xs = X_JOBS.get(u, ())
+                for tt, m in xs:
+                    if (tt, m) not in X_EARLY:
+                        transpose_x(tt, m)
                 if u < UNITS:
-                    take_squares(tt, g)
-                    if u in W_OUT_UNITS:
-                        regroup_weight(w_out_raw, "w_out", W_OUT_UNITS.index(u))
-                    if tt >= 1:
-                        add_two_squares(tt, g)
-                    if next_tile is not None and g < COMPONENTS:
-                        quantise_x(next_tile, g)
+                    take_squares(*walk[u])
+                    for g in W_JOBS.get(u, ()):
+                        if g < GROUPS:
+                            regroup_weight(w_in_raw, "w_in", g)
+                        else:
+                            regroup_weight(w_out_raw, "w_out", g - GROUPS)
+                    if u in V_ADD:
+                        add_two_squares(*walk[u])
+                    for tt, m in xs:
+                        quantise_x(tt, m)
                 if 1 <= u <= UNITS:
-                    add_squares(*units[u - 1])
+                    add_squares(*walk[u - 1])
+                for g in W_JOBS.get(u, ()):
+                    if g < GROUPS:
+                        quantise_weight(w_in_codes, w_in_scales, "w_in", g)
+                    else:
+                        quantise_weight(w_out_codes, w_out_scales, "w_out", g - GROUPS)
                 if u >= 2:
-                    take_norm(*units[u - 2])
-                if u in W_OUT_UNITS:
-                    quantise_weight(w_out_codes, w_out_scales, "w_out", W_OUT_UNITS.index(u))
-                if u == 0:
-                    regroup_weight(w_in_raw, "w_in", 3)
-                    quantise_weight(w_in_codes, w_in_scales, "w_in", 3)
+                    take_norm(*walk[u - 2])
             regroup_weight(w_out_raw, "w_out", GROUPS - 1)
             quantise_weight(w_out_codes, w_out_scales, "w_out", GROUPS - 1)
 

@@ -22,18 +22,44 @@ GROUPS = F // K_PASS
 F_TILES = F // P
 D_PIECES = D // P
 UNITS = TOKEN_TILES * GROUPS
-BANKS = 8
-HIDDEN_BANKS = 5
 MAX_INVERSE_NORM = 1e12
 RUN = 4
 RUNS = P // RUN
 GPSIMD_RUN = 3
-X_EARLY = ((1, 0), (1, 1), (1, 2))
-X_ON_SCALAR = ((0, 0), (0, 1), (0, 2))
-WALK = [(0, 0), (0, 1), (1, 0), (1, 1), (0, 2), (1, 2), (0, 3), (1, 3), (2, 0), (2, 1), (2, 2), (2, 3), (3, 0), (3, 1), (3, 2), (3, 3)]
-X_JOBS = {0: [(1, 0), (1, 1), (1, 2)], 4: [(2, 0)], 5: [(2, 1)], 6: [(2, 2)], 8: [(3, 0)], 9: [(3, 1)], 10: [(3, 2)]}
-W_JOBS = {1: (2,), 2: (3,), 7: (4,), 11: (5,), 13: (6,)}
-V_ADD = (4, 5, 6, 7, 8, 9, 10, 11, 12, 13, 14, 15)
+EARLY_UNITS = 10
+ORDER_ = (0, 2, 1)
+ADDS = (4, 5, 6, 7, 8, 9)
+WALK = [(0, 0), (0, 1), (1, 0), (1, 1), (0, 2), (1, 2), (0, 3), (1, 3), (2, 0), (2, 1)]
+X_AT = {3: (2, 0), 4: (2, 1), 5: (2, 2), 6: (3, 0), 7: (3, 1), 8: (3, 2)}
+X1_BANKS = (2, 6, 7)
+W_IN_AT = {1: (2,), 2: (3,)}
+GAP_SQUARES = 3
+TOKEN_1 = (3, 4, 5, 0)
+X_1 = 2
+SUM = (6, 7)
+CHANNEL = (0, 1, 2)
+TOKEN_2 = (3, 4, 5)
+PIECES_2 = {8: 1, 9: 2}
+W_OUT_1 = {6: (0,)}
+W_OUT_BUFS = 1
+W_PARTS = {3: (0, 1), 4: (2,), 5: (3,)}
+W_OUT_GAP = (1,)
+W_OUT_GAP2 = (2,)
+FINAL = (3, 4, 5, 6, 7, 0, 1, 2)
+T_AT = {1: 10, 3: 11, 5: 12, 6: 13, 7: 14, 8: 15}
+SQ_AT = {2: 11, 4: 12, 5: 13, 6: 14, 7: 15}
+ROOT_AT = {4: (10, 11), 5: (12,), 6: (13,), 7: (14,), 8: (15,)}
+ROOT_FIRST = (4,)
+MM_AT = {0: 11, 3: 12, 4: 13, 5: 14, 6: 15}
+GELUS = {0: (2, 3), 1: (4, 5), 2: (6, 7), 3: (8, 9)}
+LATE_GELUS = {8: (10, 11)}
+W_R_2 = {1: (3,)}
+SUM_1 = (6, 7, 1)
+SUM_2 = {10: 6, 11: 7, 12: 6, 13: 7, 14: 6, 15: 7}
+OUT_BANK = {8: (3,), 9: (3, 4)}
+PIECES_3 = {10: 1, 11: 2, 12: 2, 13: 2, 14: 1, 15: 1}
+ADD_FIRST = ()
+ADD_LAST = ()
 FLOPS = 2 * 2 * TOKEN_TILES * P * COMPONENTS * D * F
 
 
@@ -47,6 +73,7 @@ def tile_feedforwardse3_pa_kernel(tc, x, w_in, scale, bias, w_out, out):
     with ExitStack() as ctx:
         keep = ctx.enter_context(tc.tile_pool(name="keep", bufs=1))
         stage = ctx.enter_context(tc.tile_pool(name="stage", bufs=2))
+        psum = ctx.enter_context(tc.psum_pool(name="psum", bufs=1))
         ctx.enter_context(tc.manual_schedule())
 
         identity = keep.tile([P, P], BF16)
@@ -98,6 +125,15 @@ def tile_feedforwardse3_pa_kernel(tc, x, w_in, scale, bias, w_out, out):
                 in_=raw[g][:].rearrange("p j (c i) -> p c j i", i=4),
             )
 
+        def regroup_w_out(g, part):
+            if part == 0:
+                w_grouped["w_out", g] = stage.tile([P, K_PASS, PACK], BF16, align_bytes=64, name="w_out_grouped", bufs=W_OUT_BUFS)
+            cols = slice(part * P, (part + 1) * P)
+            nc.vector.tensor_copy(
+                out=w_grouped["w_out", g][:, cols, :].rearrange("p (c i) j -> p c j i", i=4),
+                in_=w_out_raw[g][:, :, cols].rearrange("p j (c i) -> p c j i", i=4),
+            )
+
         def quantise_weight(codes, scales, name, g):
             codes[g] = keep.tile([P, K_PASS], U32, align_bytes=64, name="%s_codes%d" % (name, g))
             scales[g] = keep.tile([P, K_PASS], U8, align_bytes=64, name="%s_scales%d" % (name, g))
@@ -109,14 +145,17 @@ def tile_feedforwardse3_pa_kernel(tc, x, w_in, scale, bias, w_out, out):
         x_codes = {}
         x_scales = {}
 
-        def transpose_x(tt, m):
+        def transpose_x(tt, m, bank):
             x_dm = x_raw[tt][:].rearrange("p (d m) -> p d m", m=COMPONENTS)
             x_grouped[tt, m] = stage.tile([P, P, PACK], BF16, align_bytes=64, name="x_grouped%d" % m)
-            x_t = psum.tile([P, PACK, P], BF16, tag="hidden" if tt == 0 else "sum_squares" if tt == 1 and m >= 1 and X_EARLY else "turned", bufs=HIDDEN_BANKS if tt == 0 else 2 if tt == 1 and m >= 1 and X_EARLY else 1)
+            x_t = psum.tile([P, PACK, P], BF16, tag=bank)
             for c in range(PACK):
                 nc.tensor.transpose(x_t[:, c, :], x_dm[:, c * P : (c + 1) * P, m], identity[:])
-            copy = nc.scalar.copy if (tt, m) in X_ON_SCALAR else nc.vector.tensor_copy
-            copy(out=x_grouped[tt, m][:].rearrange("p (c i) j -> p c i j", i=RUN), in_=x_t[:].rearrange("p j (i c) -> p c i j", i=RUN))
+            copy = nc.scalar.copy if tt == 0 else nc.vector.tensor_copy
+            copy(
+                out=x_grouped[tt, m][:].rearrange("p (c i) j -> p c i j", i=RUN),
+                in_=x_t[:].rearrange("p j (i c) -> p c i j", i=RUN),
+            )
 
         def quantise_x(tt, m):
             if m == 0:
@@ -128,8 +167,8 @@ def tile_feedforwardse3_pa_kernel(tc, x, w_in, scale, bias, w_out, out):
                 in_=x_grouped[tt, m][:].rearrange("p t c -> p (t c)"),
             )
 
-        def hidden(tt, g, m):
-            h = psum_2.tile([P, PACK, P], F32, tag="hidden", bufs=6)
+        def hidden(tt, g, m, bank):
+            h = psum.tile([P, PACK, P], F32, tag=bank)
             for j in range(PACK):
                 cols = slice(j * P, (j + 1) * P)
                 nc.tensor.matmul_mx(
@@ -153,42 +192,37 @@ def tile_feedforwardse3_pa_kernel(tc, x, w_in, scale, bias, w_out, out):
 
         token_hidden = {}
 
-        def hidden_by_token(tt, g):
-            token_hidden[tt, g] = []
-            for m in range(COMPONENTS):
-                h = psum.tile([P, K_PASS], F32, tag="hidden", bufs=HIDDEN_BANKS)
-                token_hidden[tt, g].append(h)
-                nc.tensor.matmul_mx(
-                    out=h[:],
-                    lhsT=x_codes[tt][:, m, :].bitcast(FP8X4),
-                    lhsT_scale=x_scales[tt][:, m, :],
-                    rhs=w_in_codes[g][:].bitcast(FP8X4),
-                    rhs_scale=w_in_scales[g][:],
-                    start=True,
-                    stop=True,
-                )
+        def hidden_by_token(tt, g, m, bank):
+            h = psum.tile([P, K_PASS], F32, tag=bank)
+            token_hidden[tt, g, m] = h
+            nc.tensor.matmul_mx(
+                out=h[:],
+                lhsT=x_codes[tt][:, m, :].bitcast(FP8X4),
+                lhsT_scale=x_scales[tt][:, m, :],
+                rhs=w_in_codes[g][:].bitcast(FP8X4),
+                rhs_scale=w_in_scales[g][:],
+                start=True,
+                stop=True,
+            )
 
-        def take_squares(tt, g):
-            squares[tt, g] = []
-            for m in range(COMPONENTS):
-                square = stage.tile([P, K_PASS], F32, name="square%d" % m, bufs=3)
-                squares[tt, g].append(square)
-                nc.scalar.activation(out=square[:], in_=token_hidden[tt, g][m][:], func=ACT.Square)
+        def take_square(tt, g, m):
+            squares[tt, g, m] = stage.tile([P, K_PASS], F32, name="square%d" % m, bufs=3)
+            nc.scalar.activation(out=squares[tt, g, m][:], in_=token_hidden[tt, g, m][:], func=ACT.Square)
 
         two_squares = {}
 
         def add_two_squares(tt, g):
             two_squares[tt, g] = stage.tile([P, K_PASS], F32, name="two_squares", bufs=3)
             nc.vector.tensor_tensor(
-                out=two_squares[tt, g][:], in0=squares[tt, g][0][:], in1=squares[tt, g][1][:], op=ALU.add
+                out=two_squares[tt, g][:], in0=squares[tt, g, 0][:], in1=squares[tt, g, 1][:], op=ALU.add
             )
 
-        def add_squares(tt, g):
-            if (tt, g) in walk[UNITS - 2 :]:
-                sum_squares[tt, g] = psum.tile([P, RUNS, PACK, RUN], F32, tag="hidden", bufs=HIDDEN_BANKS, name="last_sums")
+        def add_squares(tt, g, bank):
+            sum_squares[tt, g] = psum.tile([P, RUNS, PACK, RUN], F32, tag=bank, name="sum_squares")
+            if (tt, g) in two_squares:
+                addends = [two_squares[tt, g], squares[tt, g, 2]]
             else:
-                sum_squares[tt, g] = psum.tile([P, RUNS, PACK, RUN], F32, bufs=2, name="sum_squares")
-            addends = [two_squares[tt, g], squares[tt, g][2]] if (tt, g) in two_squares else squares[tt, g]
+                addends = [squares[tt, g, m] for m in range(COMPONENTS)]
             for j in range(PACK):
                 for addend in addends:
                     nc.tensor.matmul(
@@ -200,10 +234,12 @@ def tile_feedforwardse3_pa_kernel(tc, x, w_in, scale, bias, w_out, out):
                         stop=addend is addends[-1],
                     )
 
-        def take_norm(tt, g):
-            inverse_norm[tt, g] = stage.tile([P, RUNS, PACK, RUN], F32, name="inverse_norm", bufs=UNITS)
+        def take_inverse_norm(tt, g):
+            inverse_norm[tt, g] = stage.tile([P, RUNS, PACK, RUN], F32, name="inverse_norm", bufs=14)
             nc.scalar.activation(out=inverse_norm[tt, g][:], in_=sum_squares[tt, g][:], func=ACT.Abs_reciprocal_sqrt)
-            norm[tt, g] = stage.tile([P, RUNS, PACK, RUN], F32, name="norm", bufs=UNITS)
+
+        def take_norm(tt, g):
+            norm[tt, g] = stage.tile([P, RUNS, PACK, RUN], F32, name="norm", bufs=12)
             nc.vector.scalar_tensor_tensor(
                 out=norm[tt, g][:],
                 in0=inverse_norm[tt, g][:],
@@ -214,7 +250,7 @@ def tile_feedforwardse3_pa_kernel(tc, x, w_in, scale, bias, w_out, out):
             )
 
         def take_gelu(tt, g):
-            gelu[tt, g] = stage.tile([P, RUNS, PACK, RUN], F32, name="gelu", bufs=4)
+            gelu[tt, g] = stage.tile([P, RUNS, PACK, RUN], F32, name="gelu", bufs=8)
             for j in range(PACK):
                 ft = g * PACK + j
                 nc.scalar.activation(
@@ -242,9 +278,8 @@ def tile_feedforwardse3_pa_kernel(tc, x, w_in, scale, bias, w_out, out):
         channel_hidden = {}
         h_copy = {}
 
-        def hidden_by_channel(tt, g):
-            for m in (2, 0, 1):
-                channel_hidden[tt, g, m] = hidden(tt, g, m)
+        def hidden_by_channel(tt, g, m, bank):
+            channel_hidden[tt, g, m] = hidden(tt, g, m, bank)
 
         def copy_hidden(tt, g):
             h_copy[tt, g] = stage.tile([P, GPSIMD_RUN, RUNS, PACK], F32, name="h_copy")
@@ -270,8 +305,8 @@ def tile_feedforwardse3_pa_kernel(tc, x, w_in, scale, bias, w_out, out):
 
         def quantise_g(tt, g):
             if g == 0:
-                g_codes[tt] = stage.tile([P, GROUPS, COMPONENTS, P], U32, align_bytes=64, name="g_codes")
-                g_scales[tt] = stage.tile([P, GROUPS, COMPONENTS, P], U8, align_bytes=64, name="g_scales")
+                g_codes[tt] = stage.tile([P, GROUPS, COMPONENTS, P], U32, align_bytes=64, name="g_codes", bufs=3)
+                g_scales[tt] = stage.tile([P, GROUPS, COMPONENTS, P], U8, align_bytes=64, name="g_scales", bufs=3)
             for m in range(COMPONENTS):
                 nc.vector.quantize_mx(
                     out=g_codes[tt][:, g, m, :].bitcast(FP8X4),
@@ -281,11 +316,8 @@ def tile_feedforwardse3_pa_kernel(tc, x, w_in, scale, bias, w_out, out):
 
         accumulated = {}
 
-        def second_matmul(tt, piece, groups=range(GROUPS)):
-            if len(groups) < GROUPS:
-                acc = psum_2.tile([P, COMPONENTS, P], F32, tag="hidden", bufs=6)
-            else:
-                acc = psum_2.tile([P, COMPONENTS, P], F32, bufs=2)
+        def second_matmul(tt, piece, bank, groups=range(GROUPS)):
+            acc = psum.tile([P, COMPONENTS, P], F32, tag=bank, name="acc")
             cols = slice(piece * P, (piece + 1) * P)
             for m in range(COMPONENTS):
                 for g in groups:
@@ -314,92 +346,163 @@ def tile_feedforwardse3_pa_kernel(tc, x, w_in, scale, bias, w_out, out):
                 in_=out_piece[:].rearrange("p d m -> p (d m)"),
             )
 
-        with tc.psum_pool(name="psum_1", bufs=1) as psum:
-            for m in range(COMPONENTS):
-                transpose_x(0, m)
-            vector_cols = psum.tile([P, P], BF16, tag="turned")
-            nc.tensor.transpose(vector_cols[:], vector_rows[:], identity[:])
-            regroup_weight(w_in_raw, "w_in", 0)
-            quantise_x(0, 0)
-            quantise_weight(w_in_codes, w_in_scales, "w_in", 0)
-            quantise_x(0, 1)
-            quantise_x(0, 2)
-            gain_bias = keep.tile([P, 2 * F_TILES], F32)
-            regroup_weight(w_in_raw, "w_in", 1)
-            nc.vector.tensor_copy(out=gain_bias[:], in_=vector_cols[:, 0 : 2 * F_TILES])
-            quantise_weight(w_in_codes, w_in_scales, "w_in", 1)
-            units = [(tt, g) for tt in range(TOKEN_TILES) for g in range(GROUPS)]
-            walk = WALK
-            hidden_by_token(*walk[0])
-            for tt, m in X_EARLY:
-                transpose_x(tt, m)
-            for u in range(UNITS + 2):
-                if u + 1 < UNITS:
-                    hidden_by_token(*walk[u + 1])
-                xs = X_JOBS.get(u, ())
-                for tt, m in xs:
-                    if (tt, m) not in X_EARLY:
-                        transpose_x(tt, m)
-                if u < UNITS:
-                    take_squares(*walk[u])
-                    for g in W_JOBS.get(u, ()):
-                        if g < GROUPS:
-                            regroup_weight(w_in_raw, "w_in", g)
-                        else:
-                            regroup_weight(w_out_raw, "w_out", g - GROUPS)
-                    if u in V_ADD:
-                        add_two_squares(*walk[u])
-                    for tt, m in xs:
-                        quantise_x(tt, m)
-                if 1 <= u <= UNITS:
-                    add_squares(*walk[u - 1])
-                for g in W_JOBS.get(u, ()):
-                    if g < GROUPS:
-                        quantise_weight(w_in_codes, w_in_scales, "w_in", g)
-                    else:
-                        quantise_weight(w_out_codes, w_out_scales, "w_out", g - GROUPS)
-                if u >= 2:
-                    take_norm(*walk[u - 2])
-            regroup_weight(w_out_raw, "w_out", GROUPS - 1)
-            quantise_weight(w_out_codes, w_out_scales, "w_out", GROUPS - 1)
+        units = [(tt, g) for tt in range(TOKEN_TILES) for g in range(GROUPS)]
+        pieces = [(tt, piece) for tt in range(TOKEN_TILES) for piece in range(D_PIECES)]
+        ORDER = ORDER_
+        bank = ["bank%d" % i for i in range(8)]
+        token_count = [0]
 
-        with tc.psum_pool(name="psum_2", bufs=1) as psum_2:
-            pieces = [(tt, piece) for tt in range(TOKEN_TILES) for piece in range(D_PIECES)]
-            take_gelu(*units[0])
-            hidden_by_channel(*units[0])
-            copy_hidden(*units[0])
-            take_gelu(*units[1])
-            take_gate(*units[0])
-            last_tile = TOKEN_TILES - 1
-            pieces_done = 0
-            for u in range(UNITS):
-                for finished in list(accumulated):
-                    store(*finished)
-                if u + 1 < UNITS:
-                    hidden_by_channel(*units[u + 1])
-                    copy_hidden(*units[u + 1])
-                if u == UNITS - 1:
-                    quantise_g(*units[u - 1])
+        def token_banks(choice):
+            name = bank[choice[token_count[0] % len(choice)]]
+            token_count[0] = token_count[0] + 1
+            return name
+
+        for m in range(COMPONENTS):
+            transpose_x(0, m, bank[m])
+        vector_cols = psum.tile([P, P], BF16, tag=bank[7])
+        nc.tensor.transpose(vector_cols[:], vector_rows[:], identity[:])
+        regroup_weight(w_in_raw, "w_in", 0)
+        quantise_x(0, 0)
+        quantise_weight(w_in_codes, w_in_scales, "w_in", 0)
+        quantise_x(0, 1)
+        quantise_x(0, 2)
+        gain_bias = keep.tile([P, 2 * F_TILES], F32)
+        regroup_weight(w_in_raw, "w_in", 1)
+        nc.vector.tensor_copy(out=gain_bias[:], in_=vector_cols[:, 0 : 2 * F_TILES])
+        quantise_weight(w_in_codes, w_in_scales, "w_in", 1)
+
+        N = EARLY_UNITS
+        walk = WALK + units[N:]
+        for m in range(COMPONENTS):
+            hidden_by_token(*walk[0], m, token_banks(TOKEN_1))
+        for m in range(COMPONENTS):
+            transpose_x(1, m, bank[X1_BANKS[m]])
+        for u in range(N):
+            if u + 1 < N:
                 for m in range(COMPONENTS):
-                    multiply_by_gate(*units[u], m)
-                if u + 2 < UNITS:
-                    take_gelu(*units[u + 2])
-                if u + 1 < UNITS:
-                    take_gate(*units[u + 1])
-                if 1 <= u < UNITS - 1:
-                    quantise_g(*units[u - 1])
-                if u > GROUPS:
-                    for piece in pieces[pieces_done : pieces_done + (2 if u == UNITS - GROUPS + 1 else 1)]:
-                        second_matmul(*piece)
-                        pieces_done = pieces_done + 1
+                    hidden_by_token(*walk[u + 1], m, token_banks(TOKEN_1))
+            if u in X_AT:
+                transpose_x(*X_AT[u], bank[X_1])
+            for m in range(COMPONENTS):
+                take_square(*walk[u], m)
+            for g in W_IN_AT.get(u, ()):
+                regroup_weight(w_in_raw, "w_in", g)
+            for i in W_PARTS.get(u, ()):
+                regroup_w_out(i // 4, i % 4)
+            if u in ADDS:
+                add_two_squares(*walk[u])
+            if u == 0:
+                for m in range(COMPONENTS):
+                    quantise_x(1, m)
+            if u in X_AT:
+                quantise_x(*X_AT[u])
+            if u >= 1:
+                add_squares(*walk[u - 1], bank[SUM_1[u % len(SUM_1)]])
+            for g in W_IN_AT.get(u, ()):
+                quantise_weight(w_in_codes, w_in_scales, "w_in", g)
+            for g in W_OUT_1.get(u, ()):
+                quantise_weight(w_out_codes, w_out_scales, "w_out", g)
+            if u >= 2:
+                take_inverse_norm(*walk[u - 2])
+                take_norm(*walk[u - 2])
+
+        for m in range(COMPONENTS):
+            hidden_by_token(*units[N], m, bank[TOKEN_2[m]])
+        add_squares(*walk[N - 1], bank[SUM_1[N % len(SUM_1)]])
+        take_inverse_norm(*walk[N - 2])
+        take_norm(*walk[N - 2])
+        for m in range(GAP_SQUARES):
+            take_square(*units[N], m)
+        for m in ORDER:
+            hidden_by_channel(*units[0], m, bank[CHANNEL[m]])
+        take_inverse_norm(*walk[N - 1])
+        for g in W_OUT_GAP:
+            regroup_weight(w_out_raw, "w_out", g)
+            quantise_weight(w_out_codes, w_out_scales, "w_out", g)
+        take_norm(*walk[N - 1])
+        copy_hidden(*units[0])
+        take_gelu(*units[0])
+        take_gelu(*units[1])
+        for g in W_OUT_GAP2:
+            regroup_weight(w_out_raw, "w_out", g)
+            quantise_weight(w_out_codes, w_out_scales, "w_out", g)
+        take_gate(*units[0])
+
+        done = 0
+        for a in range(N):
+            if T_AT.get(a) is not None:
+                add_squares(*units[T_AT[a]], bank[SUM_2[T_AT[a]]])
+            for u in GELUS.get(a, ()):
+                take_gelu(*units[u])
+            late = ROOT_AT.get(a, ())
+            if SQ_AT.get(a) is not None and a not in ROOT_FIRST:
+                for m in range(COMPONENTS):
+                    take_square(*units[SQ_AT[a]], m)
+            for u in late:
+                take_inverse_norm(*units[u])
+            if a in ROOT_FIRST:
+                for m in range(COMPONENTS):
+                    take_square(*units[SQ_AT[a]], m)
+            if a in ADD_FIRST:
+                add_two_squares(*units[SQ_AT[a]])
+            for m in ORDER:
+                multiply_by_gate(*units[a], m)
+                hidden_by_channel(*units[a + 1], m, bank[CHANNEL[m]])
+            if MM_AT.get(a) is not None:
+                for m in range(COMPONENTS):
+                    hidden_by_token(*units[MM_AT[a]], m, bank[TOKEN_2[m]])
+            copy_hidden(*units[a + 1])
             for finished in list(accumulated):
                 store(*finished)
-            quantise_g(*units[UNITS - 1])
-            partial = []
-            for piece in range(D_PIECES):
-                second_matmul(last_tile, piece, range(GROUPS - 1))
-                partial.append(stage.tile([P, P, COMPONENTS], F32, name="partial%d" % piece, bufs=1))
-                nc.scalar.copy(out=partial[piece][:], in_=accumulated.pop((last_tile, piece))[:].rearrange("p m d -> p d m"))
-            for piece in range(D_PIECES):
-                second_matmul(last_tile, piece, range(GROUPS - 1, GROUPS))
-                store(last_tile, piece, partial[piece])
+            for u in LATE_GELUS.get(a, ()):
+                take_gelu(*units[u])
+            for g in W_R_2.get(a, ()):
+                regroup_weight(w_out_raw, "w_out", g)
+            if a + 1 < N:
+                take_gate(*units[a + 1])
+            for g in W_R_2.get(a, ()):
+                quantise_weight(w_out_codes, w_out_scales, "w_out", g)
+            if a in ADD_LAST:
+                add_two_squares(*units[SQ_AT[a]])
+            if a >= 1:
+                quantise_g(*units[a - 1])
+            for u in late:
+                take_norm(*units[u])
+            for i in range(PIECES_2.get(a, 0)):
+                second_matmul(*pieces[done], bank[OUT_BANK[a][i]])
+                done = done + 1
+        take_gate(*units[N])
+
+        last_tile = TOKEN_TILES - 1
+        for a in range(N, UNITS):
+            for finished in list(accumulated):
+                store(*finished)
+            if a + 1 < UNITS:
+                for m in ORDER:
+                    hidden_by_channel(*units[a + 1], m, bank[CHANNEL[m] if (a + 1 - N) % 2 == 0 else TOKEN_2[m]])
+                copy_hidden(*units[a + 1])
+            if a == UNITS - 1:
+                quantise_g(*units[a - 1])
+            for m in ORDER:
+                multiply_by_gate(*units[a], m)
+            if a + 2 < UNITS:
+                take_gelu(*units[a + 2])
+            if a + 1 < UNITS:
+                take_gate(*units[a + 1])
+            if a < UNITS - 1:
+                quantise_g(*units[a - 1])
+            for piece in pieces[done : done + PIECES_3[a]]:
+                second_matmul(*piece, bank[SUM[done % 2]])
+                done = done + 1
+        for finished in list(accumulated):
+            store(*finished)
+        quantise_g(*units[UNITS - 1])
+        partial = []
+        final_banks = CHANNEL + TOKEN_2 + SUM
+        for piece in range(D_PIECES):
+            second_matmul(last_tile, piece, bank[FINAL[piece]], range(GROUPS - 1))
+            partial.append(stage.tile([P, P, COMPONENTS], F32, name="partial%d" % piece, bufs=1))
+            nc.scalar.copy(out=partial[piece][:], in_=accumulated.pop((last_tile, piece))[:].rearrange("p m d -> p d m"))
+        for piece in range(D_PIECES):
+            second_matmul(last_tile, piece, bank[FINAL[D_PIECES + piece]], range(GROUPS - 1, GROUPS))
+            store(last_tile, piece, partial[piece])

@@ -39,7 +39,7 @@ X_1 = 2
 SUM = (6, 7)
 CHANNEL = (0, 1, 2)
 TOKEN_2 = (3, 4, 5)
-PIECES_2 = {8: 1, 9: 2}
+PIECES_2 = {8: 2, 9: 2}
 W_OUT_1 = {6: (0,)}
 W_OUT_BUFS = 1
 W_PARTS = {3: (0, 1), 4: (2,), 5: (3,)}
@@ -56,10 +56,12 @@ LATE_GELUS = {8: (10, 11)}
 W_R_2 = {1: (3,)}
 SUM_1 = (6, 7, 1)
 SUM_2 = {10: 6, 11: 7, 12: 6, 13: 7, 14: 6, 15: 7}
-OUT_BANK = {8: (3,), 9: (3, 4)}
-PIECES_3 = {10: 1, 11: 2, 12: 2, 13: 2, 14: 1, 15: 1}
+OUT_BANK = {8: (3, 4), 9: (5, 3)}
+PIECES_3 = {10: 1, 11: 2, 12: 1, 13: 2, 14: 1, 15: 1}
 ADD_FIRST = ()
 ADD_LAST = ()
+GAP_WARM = 10
+WARM = {1: 1, 2: 1, 3: 1, 4: 1}
 FLOPS = 2 * 2 * TOKEN_TILES * P * COMPONENTS * D * F
 
 
@@ -167,8 +169,12 @@ def tile_feedforwardse3_pa_kernel(tc, x, w_in, scale, bias, w_out, out):
                 in_=x_grouped[tt, m][:].rearrange("p t c -> p (t c)"),
             )
 
-        def hidden(tt, g, m, bank):
+        def hidden(tt, g, m, bank, warm=0):
             h = psum.tile([P, PACK, P], F32, tag=bank)
+            for again in range(warm):
+                nc.tensor.matmul(
+                    h[:].rearrange("p j t -> p (j t)"), lhsT=identity[:], rhs=x_raw[0][:, 0:K_PASS], start=True, stop=True
+                )
             for j in range(PACK):
                 cols = slice(j * P, (j + 1) * P)
                 nc.tensor.matmul_mx(
@@ -278,8 +284,8 @@ def tile_feedforwardse3_pa_kernel(tc, x, w_in, scale, bias, w_out, out):
         channel_hidden = {}
         h_copy = {}
 
-        def hidden_by_channel(tt, g, m, bank):
-            channel_hidden[tt, g, m] = hidden(tt, g, m, bank)
+        def hidden_by_channel(tt, g, m, bank, warm=0):
+            channel_hidden[tt, g, m] = hidden(tt, g, m, bank, warm)
 
         def copy_hidden(tt, g):
             h_copy[tt, g] = stage.tile([P, GPSIMD_RUN, RUNS, PACK], F32, name="h_copy")
@@ -414,7 +420,7 @@ def tile_feedforwardse3_pa_kernel(tc, x, w_in, scale, bias, w_out, out):
         for m in range(GAP_SQUARES):
             take_square(*units[N], m)
         for m in ORDER:
-            hidden_by_channel(*units[0], m, bank[CHANNEL[m]])
+            hidden_by_channel(*units[0], m, bank[CHANNEL[m]], GAP_WARM if m == ORDER[-1] else 0)
         take_inverse_norm(*walk[N - 1])
         for g in W_OUT_GAP:
             regroup_weight(w_out_raw, "w_out", g)
@@ -447,7 +453,7 @@ def tile_feedforwardse3_pa_kernel(tc, x, w_in, scale, bias, w_out, out):
                 add_two_squares(*units[SQ_AT[a]])
             for m in ORDER:
                 multiply_by_gate(*units[a], m)
-                hidden_by_channel(*units[a + 1], m, bank[CHANNEL[m]])
+                hidden_by_channel(*units[a + 1], m, bank[CHANNEL[m]], WARM.get(a, 0) if m == ORDER[-1] else 0)
             if MM_AT.get(a) is not None:
                 for m in range(COMPONENTS):
                     hidden_by_token(*units[MM_AT[a]], m, bank[TOKEN_2[m]])

@@ -43,7 +43,7 @@ PIECES_2 = {8: 2, 9: 2}
 W_OUT_1 = {6: (0,)}
 W_OUT_BUFS = 1
 W_PARTS = {3: (0, 1), 4: (2,), 5: (3,)}
-W_OUT_GAP = (1,)
+W_OUT_GAP = ()
 W_OUT_GAP2 = (2,)
 FINAL = (3, 4, 5, 6, 7, 0, 1, 2)
 T_AT = {1: 10, 3: 11, 5: 12, 6: 13, 7: 14, 8: 15}
@@ -56,12 +56,13 @@ LATE_GELUS = {8: (10, 11)}
 W_R_2 = {1: (3,)}
 SUM_1 = (6, 7, 1)
 SUM_2 = {10: 6, 11: 7, 12: 6, 13: 7, 14: 6, 15: 7}
-OUT_BANK = {8: (3, 4), 9: (5, 3)}
-PIECES_3 = {10: 1, 11: 2, 12: 1, 13: 2, 14: 1, 15: 1}
+OUT_BANK = {8: (3, 4), 9: (5, 6)}
+PIECES_3 = {10: 1, 11: 1, 12: 2, 13: 2, 14: 1, 15: 1}
 ADD_FIRST = ()
 ADD_LAST = ()
 GAP_WARM = 10
 WARM = {1: 1, 2: 1, 3: 1, 4: 1}
+W_GAP0 = (1,)
 FLOPS = 2 * 2 * TOKEN_TILES * P * COMPONENTS * D * F
 
 
@@ -297,7 +298,7 @@ def tile_feedforwardse3_pa_kernel(tc, x, w_in, scale, bias, w_out, out):
         def multiply_by_gate(tt, g, m):
             g_grouped[tt, g, m] = stage.tile([P, RUN, RUNS, PACK], BF16, align_bytes=64, name="g_grouped%d" % m, bufs=2)
             first = 0
-            if m == COMPONENTS - 1:
+            if m == COMPONENTS - 1 and (tt, g) in h_copy:
                 first = GPSIMD_RUN
                 nc.gpsimd.tensor_tensor(
                     out=g_grouped[tt, g, m][:, 0:first], in0=h_copy[tt, g][:], in1=gate[tt, g][:, 0:first], op=ALU.mult
@@ -384,9 +385,8 @@ def tile_feedforwardse3_pa_kernel(tc, x, w_in, scale, bias, w_out, out):
         for m in range(COMPONENTS):
             transpose_x(1, m, bank[X1_BANKS[m]])
         for u in range(N):
-            if u + 1 < N:
-                for m in range(COMPONENTS):
-                    hidden_by_token(*walk[u + 1], m, token_banks(TOKEN_1))
+            for m in range(COMPONENTS):
+                hidden_by_token(*walk[u + 1], m, token_banks(TOKEN_1) if u + 1 < N else bank[TOKEN_2[m]])
             if u in X_AT:
                 transpose_x(*X_AT[u], bank[X_1])
             for m in range(COMPONENTS):
@@ -412,13 +412,15 @@ def tile_feedforwardse3_pa_kernel(tc, x, w_in, scale, bias, w_out, out):
                 take_inverse_norm(*walk[u - 2])
                 take_norm(*walk[u - 2])
 
-        for m in range(COMPONENTS):
-            hidden_by_token(*units[N], m, bank[TOKEN_2[m]])
         add_squares(*walk[N - 1], bank[SUM_1[N % len(SUM_1)]])
-        take_inverse_norm(*walk[N - 2])
-        take_norm(*walk[N - 2])
         for m in range(GAP_SQUARES):
             take_square(*units[N], m)
+        take_inverse_norm(*walk[N - 2])
+        for g in W_GAP0:
+            regroup_weight(w_out_raw, "w_out", g)
+        take_norm(*walk[N - 2])
+        for g in W_GAP0:
+            quantise_weight(w_out_codes, w_out_scales, "w_out", g)
         for m in ORDER:
             hidden_by_channel(*units[0], m, bank[CHANNEL[m]], GAP_WARM if m == ORDER[-1] else 0)
         take_inverse_norm(*walk[N - 1])
@@ -486,7 +488,8 @@ def tile_feedforwardse3_pa_kernel(tc, x, w_in, scale, bias, w_out, out):
             if a + 1 < UNITS:
                 for m in ORDER:
                     hidden_by_channel(*units[a + 1], m, bank[CHANNEL[m] if (a + 1 - N) % 2 == 0 else TOKEN_2[m]])
-                copy_hidden(*units[a + 1])
+                if a + 2 < UNITS:
+                    copy_hidden(*units[a + 1])
             if a == UNITS - 1:
                 quantise_g(*units[a - 1])
             for m in ORDER:

@@ -22,48 +22,36 @@ GROUPS = F // K_PASS
 F_TILES = F // P
 D_PIECES = D // P
 UNITS = TOKEN_TILES * GROUPS
-MAX_INVERSE_NORM = 1e12
 RUN = 4
 RUNS = P // RUN
-GPSIMD_RUN = 3
-EARLY_UNITS = 10
-ORDER_ = (0, 2, 1)
-ADDS = (4, 5, 6, 7, 8, 9)
-WALK = [(0, 0), (0, 1), (1, 0), (1, 1), (0, 2), (1, 2), (0, 3), (1, 3), (2, 0), (2, 1)]
-X_AT = {3: (2, 0), 4: (2, 1), 5: (2, 2), 6: (3, 0), 7: (3, 1), 8: (3, 2)}
-X1_BANKS = (2, 6, 7)
-W_IN_AT = {1: (2,), 2: (3,)}
-GAP_SQUARES = 3
-TOKEN_1 = (3, 4, 5, 0)
-X_1 = 2
-SUM = (6, 7)
-CHANNEL = (0, 1, 2)
-TOKEN_2 = (3, 4, 5)
-PIECES_2 = {8: 2, 9: 2}
-W_OUT_1 = {6: (0,)}
-W_OUT_BUFS = 1
-W_PARTS = {3: (0, 1), 4: (2,), 5: (3,)}
-W_OUT_GAP = ()
-W_OUT_GAP2 = (2,)
-FINAL = (3, 4, 5, 6, 7, 0, 1, 2)
-T_AT = {1: 10, 3: 11, 5: 12, 6: 13, 7: 14, 8: 15}
-SQ_AT = {2: 11, 4: 12, 5: 13, 6: 14, 7: 15}
-ROOT_AT = {4: (10, 11), 5: (12,), 6: (13,), 7: (14,), 8: (15,)}
-ROOT_FIRST = (4,)
-MM_AT = {0: 11, 3: 12, 4: 13, 5: 14, 6: 15}
-GELUS = {0: (2, 3), 1: (4, 5), 2: (6, 7), 3: (8, 9)}
-LATE_GELUS = {8: (10, 11)}
-W_R_2 = {1: (3,)}
-SUM_1 = (6, 7, 1)
-SUM_2 = {10: 6, 11: 7, 12: 6, 13: 7, 14: 6, 15: 7}
-OUT_BANK = {8: (3, 4), 9: (5, 6)}
-PIECES_3 = {10: 1, 11: 1, 12: 2, 13: 2, 14: 1, 15: 1}
-ADD_FIRST = ()
-ADD_LAST = ()
-GAP_WARM = 10
-WARM = {1: 1, 2: 1, 3: 1, 4: 1}
-W_GAP0 = (1,)
+MAX_INVERSE_NORM = 1e12
 FLOPS = 2 * 2 * TOKEN_TILES * P * COMPONENTS * D * F
+
+EARLY = 10
+EARLY_WALK = (0, 1, 4, 5, 2, 6, 3, 7, 8, 9)
+FIRST_ADD = 4
+SCALAR_COLUMNS = 256
+
+HIDDEN_AT = {0: 11, 3: 12, 4: 13, 5: 14, 6: 15}
+SQUARES_AT = {2: 11, 4: 12, 5: 13, 6: 14, 7: 15}
+SUMS_AT = {1: 10, 3: 11, 5: 12, 6: 13, 7: 14, 8: 15}
+ROOTS_AT = {4: (10, 11), 5: (12,), 6: (13,), 7: (14,), 8: (15,)}
+PIECES_AT = {8: 2, 9: 2, 10: 1, 11: 1, 12: 2, 13: 2, 14: 1, 15: 1}
+GPSIMD_RUN = 3
+WITHOUT_GPSIMD = (4, UNITS - 1)
+
+WARM_HEAD = (5, 3)
+WARM_CHANGE = 12
+WARM_STEPS = (1, 2, 3)
+
+CHANNEL_BANKS = (0, 1, 2)
+TOKEN_BANKS = (3, 4, 5)
+SUM_BANKS = (6, 7)
+EARLY_TOKEN_BANKS = (3, 4, 5, 0)
+EARLY_SUM_BANKS = (6, 7, 1)
+TURNED_BANK = 2
+X1_BANKS = (2, 6, 7)
+MERGED_PIECES = 2
 
 
 def tile_feedforwardse3_pa_kernel(tc, x, w_in, scale, bias, w_out, out):
@@ -79,10 +67,15 @@ def tile_feedforwardse3_pa_kernel(tc, x, w_in, scale, bias, w_out, out):
         psum = ctx.enter_context(tc.psum_pool(name="psum", bufs=1))
         ctx.enter_context(tc.manual_schedule())
 
+        def bank(index):
+            return "bank%d" % index
+
         identity = keep.tile([P, P], BF16)
         vector_rows = keep.tile([P, P], BF16)
         one = keep.tile([P, 1], F32)
+        zeros = keep.tile([P, K_PASS], BF16)
         nc.vector.memset(vector_rows[:], 0.0)
+        nc.vector.memset(zeros[:], 0.0)
         nc.vector.memset(one[:], 1.0)
         x_raw = {}
         w_in_raw = {}
@@ -98,14 +91,14 @@ def tile_feedforwardse3_pa_kernel(tc, x, w_in, scale, bias, w_out, out):
 
         load_x(0)
         load_weight(w_in_raw, w_in_pieces, 0, "w_in_raw")
-        nc.sync.dma_start(out=vector_rows[0:F_TILES, :], in_=scale.rearrange("a b (r c) -> (a b r) c", c=P))
-        nc.sync.dma_start(out=vector_rows[F_TILES : 2 * F_TILES, :], in_=bias.rearrange("a b (r c) -> (a b r) c", c=P))
         load_weight(w_in_raw, w_in_pieces, 1, "w_in_raw")
         load_x(1)
-        for g in range(2, GROUPS):
-            load_weight(w_in_raw, w_in_pieces, g, "w_in_raw")
-        for tt in range(2, TOKEN_TILES):
-            load_x(tt)
+        load_weight(w_in_raw, w_in_pieces, 2, "w_in_raw")
+        load_weight(w_in_raw, w_in_pieces, 3, "w_in_raw")
+        load_x(2)
+        load_x(3)
+        nc.sync.dma_start(out=vector_rows[0:F_TILES, :], in_=scale.rearrange("a b (r c) -> (a b r) c", c=P))
+        nc.sync.dma_start(out=vector_rows[F_TILES : 2 * F_TILES, :], in_=bias.rearrange("a b (r c) -> (a b r) c", c=P))
         for g in range(GROUPS):
             load_weight(w_out_raw, w_out_pieces, g, "w_out_raw")
 
@@ -121,21 +114,17 @@ def tile_feedforwardse3_pa_kernel(tc, x, w_in, scale, bias, w_out, out):
         w_out_codes = {}
         w_out_scales = {}
 
-        def regroup_weight(raw, name, g):
-            w_grouped[name, g] = stage.tile([P, K_PASS, PACK], BF16, align_bytes=64, name="w_grouped")
-            nc.vector.tensor_copy(
-                out=w_grouped[name, g][:].rearrange("p (c i) j -> p c j i", i=4),
-                in_=raw[g][:].rearrange("p j (c i) -> p c j i", i=4),
+        def regroup_columns(copy, raw, name, g, first, last):
+            copy(
+                out=w_grouped[name, g][:, first:last].rearrange("p (c i) j -> p c j i", i=4),
+                in_=raw[g][:, :, first:last].rearrange("p j (c i) -> p c j i", i=4),
             )
 
-        def regroup_w_out(g, part):
-            if part == 0:
-                w_grouped["w_out", g] = stage.tile([P, K_PASS, PACK], BF16, align_bytes=64, name="w_out_grouped", bufs=W_OUT_BUFS)
-            cols = slice(part * P, (part + 1) * P)
-            nc.vector.tensor_copy(
-                out=w_grouped["w_out", g][:, cols, :].rearrange("p (c i) j -> p c j i", i=4),
-                in_=w_out_raw[g][:, :, cols].rearrange("p j (c i) -> p c j i", i=4),
-            )
+        def regroup_weight(raw, name, g, scalar_columns=0):
+            w_grouped[name, g] = stage.tile([P, K_PASS, PACK], BF16, align_bytes=64, name="w_grouped")
+            if scalar_columns > 0:
+                regroup_columns(nc.scalar.copy, raw, name, g, 0, scalar_columns)
+            regroup_columns(nc.vector.tensor_copy, raw, name, g, scalar_columns, K_PASS)
 
         def quantise_weight(codes, scales, name, g):
             codes[g] = keep.tile([P, K_PASS], U32, align_bytes=64, name="%s_codes%d" % (name, g))
@@ -144,16 +133,28 @@ def tile_feedforwardse3_pa_kernel(tc, x, w_in, scale, bias, w_out, out):
                 out=codes[g][:].bitcast(FP8X4), scales=scales[g][:], in_=w_grouped[name, g][:].rearrange("p w j -> p (w j)")
             )
 
+        def regroup_w_in(g, scalar_columns=0):
+            regroup_weight(w_in_raw, "w_in", g, scalar_columns)
+
+        def quantise_w_in(g):
+            quantise_weight(w_in_codes, w_in_scales, "w_in", g)
+
+        def regroup_w_out(g):
+            regroup_weight(w_out_raw, "w_out", g)
+
+        def quantise_w_out(g):
+            quantise_weight(w_out_codes, w_out_scales, "w_out", g)
+
         x_grouped = {}
         x_codes = {}
         x_scales = {}
 
-        def transpose_x(tt, m, bank):
+        def transpose_x(tt, m, bank_index):
             x_dm = x_raw[tt][:].rearrange("p (d m) -> p d m", m=COMPONENTS)
             x_grouped[tt, m] = stage.tile([P, P, PACK], BF16, align_bytes=64, name="x_grouped%d" % m)
-            x_t = psum.tile([P, PACK, P], BF16, tag=bank)
-            for c in range(PACK):
-                nc.tensor.transpose(x_t[:, c, :], x_dm[:, c * P : (c + 1) * P, m], identity[:])
+            x_t = psum.tile([P, PACK, P], BF16, tag=bank(bank_index))
+            for j in range(PACK):
+                nc.tensor.transpose(x_t[:, j, :], x_dm[:, j * P : (j + 1) * P, m], identity[:])
             copy = nc.scalar.copy if tt == 0 else nc.vector.tensor_copy
             copy(
                 out=x_grouped[tt, m][:].rearrange("p (c i) j -> p c i j", i=RUN),
@@ -167,11 +168,105 @@ def tile_feedforwardse3_pa_kernel(tc, x, w_in, scale, bias, w_out, out):
             nc.vector.quantize_mx(
                 out=x_codes[tt][:, m, :].bitcast(FP8X4),
                 scales=x_scales[tt][:, m, :],
-                in_=x_grouped[tt, m][:].rearrange("p t c -> p (t c)"),
+                in_=x_grouped[tt, m][:].rearrange("p t j -> p (t j)"),
             )
 
-        def hidden(tt, g, m, bank, warm=0):
-            h = psum.tile([P, PACK, P], F32, tag=bank)
+        token_hidden = {}
+        squares = {}
+        two_squares = {}
+        sum_squares = {}
+        inverse_norm = {}
+        norm = {}
+
+        def hidden_by_token(u, m, bank_index):
+            tt, g = u // GROUPS, u % GROUPS
+            token_hidden[u, m] = psum.tile([P, K_PASS], F32, tag=bank(bank_index), name="token_hidden")
+            nc.tensor.matmul_mx(
+                out=token_hidden[u, m][:],
+                lhsT=x_codes[tt][:, m, :].bitcast(FP8X4),
+                lhsT_scale=x_scales[tt][:, m, :],
+                rhs=w_in_codes[g][:].bitcast(FP8X4),
+                rhs_scale=w_in_scales[g][:],
+                start=True,
+                stop=True,
+            )
+
+        def take_squares(u):
+            for m in range(COMPONENTS):
+                squares[u, m] = stage.tile([P, K_PASS], F32, name="square%d" % m, bufs=3)
+                nc.scalar.activation(out=squares[u, m][:], in_=token_hidden[u, m][:], func=ACT.Square)
+
+        def add_two_squares(u):
+            two_squares[u] = stage.tile([P, K_PASS], F32, name="two_squares", bufs=3)
+            nc.vector.tensor_tensor(out=two_squares[u][:], in0=squares[u, 0][:], in1=squares[u, 1][:], op=ALU.add)
+
+        def add_squares(u, bank_index):
+            sum_squares[u] = psum.tile([P, RUNS, PACK, RUN], F32, tag=bank(bank_index), name="sum_squares")
+            if u in two_squares:
+                addends = (two_squares[u], squares[u, 2])
+            else:
+                addends = tuple(squares[u, m] for m in range(COMPONENTS))
+            for j in range(PACK):
+                for k in range(len(addends)):
+                    nc.tensor.matmul(
+                        sum_squares[u][:, :, j, :],
+                        lhsT=addends[k][:, j * P : (j + 1) * P],
+                        rhs=identity_f32[:],
+                        is_transpose=True,
+                        start=(k == 0),
+                        stop=(k == len(addends) - 1),
+                    )
+
+        def take_root(u):
+            inverse_norm[u] = stage.tile([P, RUNS, PACK, RUN], F32, name="inverse_norm", bufs=14)
+            nc.scalar.activation(out=inverse_norm[u][:], in_=sum_squares[u][:], func=ACT.Abs_reciprocal_sqrt)
+
+        def take_norm(u):
+            norm[u] = stage.tile([P, RUNS, PACK, RUN], F32, name="norm", bufs=12)
+            nc.vector.scalar_tensor_tensor(
+                out=norm[u][:],
+                in0=inverse_norm[u][:],
+                scalar=MAX_INVERSE_NORM,
+                in1=sum_squares[u][:],
+                op0=ALU.min,
+                op1=ALU.mult,
+            )
+
+        gelu = {}
+        gate = {}
+        channel_hidden = {}
+        h_copy = {}
+        g_grouped = {}
+        g_codes = {}
+        g_scales = {}
+        component_order = (0, 2, 1)
+
+        def take_gelu(u):
+            gelu[u] = stage.tile([P, RUNS, PACK, RUN], F32, name="gelu", bufs=8)
+            for j in range(PACK):
+                ft = u % GROUPS * PACK + j
+                nc.scalar.activation(
+                    out=gelu[u][:, :, j, :],
+                    in_=norm[u][:, :, j, :],
+                    func=ACT.Gelu,
+                    bias=gain_bias[:, F_TILES + ft : F_TILES + ft + 1],
+                    scale=gain_bias[:, ft : ft + 1],
+                )
+
+        def take_gate(u):
+            gate[u] = stage.tile([P, RUN, RUNS, PACK], F32, name="gate", bufs=3)
+            nc.vector.scalar_tensor_tensor(
+                out=gate[u][:].rearrange("p i c j -> p (c j) i"),
+                in0=inverse_norm[u][:].rearrange("p c j i -> p (c j) i"),
+                scalar=MAX_INVERSE_NORM,
+                in1=gelu[u][:].rearrange("p c j i -> p (c j) i"),
+                op0=ALU.min,
+                op1=ALU.mult,
+            )
+
+        def hidden_by_channel(u, m, bank_index, warm=0):
+            tt, g = u // GROUPS, u % GROUPS
+            h = psum.tile([P, PACK, P], F32, tag=bank(bank_index))
             for again in range(warm):
                 nc.tensor.matmul(
                     h[:].rearrange("p j t -> p (j t)"), lhsT=identity[:], rhs=x_raw[0][:, 0:K_PASS], start=True, stop=True
@@ -187,130 +282,26 @@ def tile_feedforwardse3_pa_kernel(tc, x, w_in, scale, bias, w_out, out):
                     start=True,
                     stop=True,
                 )
-            return h
+            channel_hidden[u, m] = h[:].rearrange("p j (c i) -> p i c j", i=RUN)
 
-        squares = {}
-        sum_squares = {}
-        inverse_norm = {}
-        norm = {}
-        gelu = {}
-        g_codes = {}
-        g_scales = {}
+        def copy_hidden(u):
+            h_copy[u] = stage.tile([P, GPSIMD_RUN, RUNS, PACK], F32, name="h_copy")
+            nc.scalar.copy(out=h_copy[u][:], in_=channel_hidden[u, COMPONENTS - 1][:, 0:GPSIMD_RUN])
 
-        token_hidden = {}
-
-        def hidden_by_token(tt, g, m, bank):
-            h = psum.tile([P, K_PASS], F32, tag=bank)
-            token_hidden[tt, g, m] = h
-            nc.tensor.matmul_mx(
-                out=h[:],
-                lhsT=x_codes[tt][:, m, :].bitcast(FP8X4),
-                lhsT_scale=x_scales[tt][:, m, :],
-                rhs=w_in_codes[g][:].bitcast(FP8X4),
-                rhs_scale=w_in_scales[g][:],
-                start=True,
-                stop=True,
-            )
-
-        def take_square(tt, g, m):
-            squares[tt, g, m] = stage.tile([P, K_PASS], F32, name="square%d" % m, bufs=3)
-            nc.scalar.activation(out=squares[tt, g, m][:], in_=token_hidden[tt, g, m][:], func=ACT.Square)
-
-        two_squares = {}
-
-        def add_two_squares(tt, g):
-            two_squares[tt, g] = stage.tile([P, K_PASS], F32, name="two_squares", bufs=3)
-            nc.vector.tensor_tensor(
-                out=two_squares[tt, g][:], in0=squares[tt, g, 0][:], in1=squares[tt, g, 1][:], op=ALU.add
-            )
-
-        def add_squares(tt, g, bank):
-            sum_squares[tt, g] = psum.tile([P, RUNS, PACK, RUN], F32, tag=bank, name="sum_squares")
-            if (tt, g) in two_squares:
-                addends = [two_squares[tt, g], squares[tt, g, 2]]
-            else:
-                addends = [squares[tt, g, m] for m in range(COMPONENTS)]
-            for j in range(PACK):
-                for addend in addends:
-                    nc.tensor.matmul(
-                        sum_squares[tt, g][:, :, j, :],
-                        lhsT=addend[:, j * P : (j + 1) * P],
-                        rhs=identity_f32[:],
-                        is_transpose=True,
-                        start=addend is addends[0],
-                        stop=addend is addends[-1],
-                    )
-
-        def take_inverse_norm(tt, g):
-            inverse_norm[tt, g] = stage.tile([P, RUNS, PACK, RUN], F32, name="inverse_norm", bufs=14)
-            nc.scalar.activation(out=inverse_norm[tt, g][:], in_=sum_squares[tt, g][:], func=ACT.Abs_reciprocal_sqrt)
-
-        def take_norm(tt, g):
-            norm[tt, g] = stage.tile([P, RUNS, PACK, RUN], F32, name="norm", bufs=12)
-            nc.vector.scalar_tensor_tensor(
-                out=norm[tt, g][:],
-                in0=inverse_norm[tt, g][:],
-                scalar=MAX_INVERSE_NORM,
-                in1=sum_squares[tt, g][:],
-                op0=ALU.min,
-                op1=ALU.mult,
-            )
-
-        def take_gelu(tt, g):
-            gelu[tt, g] = stage.tile([P, RUNS, PACK, RUN], F32, name="gelu", bufs=8)
-            for j in range(PACK):
-                ft = g * PACK + j
-                nc.scalar.activation(
-                    out=gelu[tt, g][:, :, j, :],
-                    in_=norm[tt, g][:, :, j, :],
-                    func=ACT.Gelu,
-                    bias=gain_bias[:, F_TILES + ft : F_TILES + ft + 1],
-                    scale=gain_bias[:, ft : ft + 1],
-                )
-
-        gate = {}
-        g_grouped = {}
-
-        def take_gate(tt, g):
-            gate[tt, g] = stage.tile([P, RUN, RUNS, PACK], F32, name="gate", bufs=3)
-            nc.vector.scalar_tensor_tensor(
-                out=gate[tt, g][:].rearrange("p i c j -> p (c j) i"),
-                in0=inverse_norm[tt, g][:].rearrange("p c j i -> p (c j) i"),
-                scalar=MAX_INVERSE_NORM,
-                in1=gelu[tt, g][:].rearrange("p c j i -> p (c j) i"),
-                op0=ALU.min,
-                op1=ALU.mult,
-            )
-
-        channel_hidden = {}
-        h_copy = {}
-
-        def hidden_by_channel(tt, g, m, bank, warm=0):
-            channel_hidden[tt, g, m] = hidden(tt, g, m, bank, warm)
-
-        def copy_hidden(tt, g):
-            h_copy[tt, g] = stage.tile([P, GPSIMD_RUN, RUNS, PACK], F32, name="h_copy")
-            nc.scalar.copy(
-                out=h_copy[tt, g][:],
-                in_=channel_hidden[tt, g, COMPONENTS - 1][:].rearrange("p j (c i) -> p i c j", i=RUN)[:, 0:GPSIMD_RUN],
-            )
-
-        def multiply_by_gate(tt, g, m):
-            g_grouped[tt, g, m] = stage.tile([P, RUN, RUNS, PACK], BF16, align_bytes=64, name="g_grouped%d" % m, bufs=2)
+        def multiply_by_gate(u, m):
+            g_grouped[u, m] = stage.tile([P, RUN, RUNS, PACK], BF16, align_bytes=64, name="g_grouped%d" % m, bufs=2)
             first = 0
-            if m == COMPONENTS - 1 and (tt, g) in h_copy:
+            if m == COMPONENTS - 1 and u in h_copy:
                 first = GPSIMD_RUN
                 nc.gpsimd.tensor_tensor(
-                    out=g_grouped[tt, g, m][:, 0:first], in0=h_copy[tt, g][:], in1=gate[tt, g][:, 0:first], op=ALU.mult
+                    out=g_grouped[u, m][:, 0:first], in0=h_copy[u][:], in1=gate[u][:, 0:first], op=ALU.mult
                 )
             nc.vector.tensor_tensor(
-                out=g_grouped[tt, g, m][:, first:],
-                in0=channel_hidden[tt, g, m][:].rearrange("p j (c i) -> p i c j", i=RUN)[:, first:],
-                in1=gate[tt, g][:, first:],
-                op=ALU.mult,
+                out=g_grouped[u, m][:, first:], in0=channel_hidden[u, m][:, first:], in1=gate[u][:, first:], op=ALU.mult
             )
 
-        def quantise_g(tt, g):
+        def quantise_g(u):
+            tt, g = u // GROUPS, u % GROUPS
             if g == 0:
                 g_codes[tt] = stage.tile([P, GROUPS, COMPONENTS, P], U32, align_bytes=64, name="g_codes", bufs=3)
                 g_scales[tt] = stage.tile([P, GROUPS, COMPONENTS, P], U8, align_bytes=64, name="g_scales", bufs=3)
@@ -318,13 +309,13 @@ def tile_feedforwardse3_pa_kernel(tc, x, w_in, scale, bias, w_out, out):
                 nc.vector.quantize_mx(
                     out=g_codes[tt][:, g, m, :].bitcast(FP8X4),
                     scales=g_scales[tt][:, g, m, :],
-                    in_=g_grouped[tt, g, m][:].rearrange("p i c j -> p (i c j)"),
+                    in_=g_grouped[u, m][:].rearrange("p i c j -> p (i c j)"),
                 )
 
-        accumulated = {}
+        waiting = []
 
-        def second_matmul(tt, piece, bank, groups=range(GROUPS)):
-            acc = psum.tile([P, COMPONENTS, P], F32, tag=bank, name="acc")
+        def second_matmul(tt, piece, bank_index, groups):
+            acc = psum.tile([P, COMPONENTS, P], F32, tag=bank(bank_index), name="acc")
             cols = slice(piece * P, (piece + 1) * P)
             for m in range(COMPONENTS):
                 for g in groups:
@@ -337,181 +328,171 @@ def tile_feedforwardse3_pa_kernel(tc, x, w_in, scale, bias, w_out, out):
                         start=(g == groups[0]),
                         stop=(g == groups[-1]),
                     )
-            accumulated[tt, piece] = acc
+            return acc[:].rearrange("p m d -> p d m")
 
-        def store(tt, piece, partial=None):
+        def store(tt, piece, acc, partial=None):
             out_piece = stage.tile([P, P, COMPONENTS], F32, bufs=4)
-            acc = accumulated.pop((tt, piece))
             if partial is None:
-                nc.scalar.copy(out=out_piece[:], in_=acc[:].rearrange("p m d -> p d m"))
+                nc.scalar.copy(out=out_piece[:], in_=acc)
             else:
-                nc.vector.tensor_tensor(
-                    out=out_piece[:], in0=acc[:].rearrange("p m d -> p d m"), in1=partial[:], op=ALU.add
-                )
+                nc.vector.tensor_tensor(out=out_piece[:], in0=acc, in1=partial[:], op=ALU.add)
             nc.sync.dma_start(
                 out=out_rows[tt][:, piece * P * COMPONENTS : (piece + 1) * P * COMPONENTS],
                 in_=out_piece[:].rearrange("p d m -> p (d m)"),
             )
 
-        units = [(tt, g) for tt in range(TOKEN_TILES) for g in range(GROUPS)]
-        pieces = [(tt, piece) for tt in range(TOKEN_TILES) for piece in range(D_PIECES)]
-        ORDER = ORDER_
-        bank = ["bank%d" % i for i in range(8)]
-        token_count = [0]
+        def store_waiting():
+            for tt, piece, acc in waiting:
+                store(tt, piece, acc)
+            waiting.clear()
 
-        def token_banks(choice):
-            name = bank[choice[token_count[0] % len(choice)]]
-            token_count[0] = token_count[0] + 1
-            return name
+        def keep_warm(bank_index, count):
+            idle = psum.tile([P, K_PASS], F32, tag=bank(bank_index), name="idle")
+            for again in range(count):
+                nc.tensor.matmul(idle[:], lhsT=zeros[:, 0:P], rhs=zeros[:], start=True, stop=True)
 
+        keep_warm(TOKEN_BANKS[0], WARM_HEAD[0])
         for m in range(COMPONENTS):
-            transpose_x(0, m, bank[m])
-        vector_cols = psum.tile([P, P], BF16, tag=bank[7])
-        nc.tensor.transpose(vector_cols[:], vector_rows[:], identity[:])
-        regroup_weight(w_in_raw, "w_in", 0)
+            transpose_x(0, m, CHANNEL_BANKS[m])
+        keep_warm(TOKEN_BANKS[0], WARM_HEAD[1])
+        regroup_w_in(0)
         quantise_x(0, 0)
-        quantise_weight(w_in_codes, w_in_scales, "w_in", 0)
+        quantise_w_in(0)
         quantise_x(0, 1)
         quantise_x(0, 2)
-        gain_bias = keep.tile([P, 2 * F_TILES], F32)
-        regroup_weight(w_in_raw, "w_in", 1)
-        nc.vector.tensor_copy(out=gain_bias[:], in_=vector_cols[:, 0 : 2 * F_TILES])
-        quantise_weight(w_in_codes, w_in_scales, "w_in", 1)
+        regroup_w_in(1, SCALAR_COLUMNS)
+        quantise_w_in(1)
 
-        N = EARLY_UNITS
-        walk = WALK + units[N:]
+        token_banks = [
+            EARLY_TOKEN_BANKS[(COMPONENTS * k + m) % len(EARLY_TOKEN_BANKS)] for k in range(EARLY) for m in range(COMPONENTS)
+        ] + list(TOKEN_BANKS)
+        walk = list(EARLY_WALK) + [EARLY]
         for m in range(COMPONENTS):
-            hidden_by_token(*walk[0], m, token_banks(TOKEN_1))
+            hidden_by_token(walk[0], m, token_banks[m])
         for m in range(COMPONENTS):
-            transpose_x(1, m, bank[X1_BANKS[m]])
-        for u in range(N):
+            transpose_x(1, m, X1_BANKS[m])
+        for k in range(EARLY):
             for m in range(COMPONENTS):
-                hidden_by_token(*walk[u + 1], m, token_banks(TOKEN_1) if u + 1 < N else bank[TOKEN_2[m]])
-            if u in X_AT:
-                transpose_x(*X_AT[u], bank[X_1])
-            for m in range(COMPONENTS):
-                take_square(*walk[u], m)
-            for g in W_IN_AT.get(u, ()):
-                regroup_weight(w_in_raw, "w_in", g)
-            for i in W_PARTS.get(u, ()):
-                regroup_w_out(i // 4, i % 4)
-            if u in ADDS:
-                add_two_squares(*walk[u])
-            if u == 0:
+                hidden_by_token(walk[k + 1], m, token_banks[COMPONENTS * (k + 1) + m])
+            x_job = divmod(k - 3, COMPONENTS)
+            if 0 <= x_job[0] < 2:
+                transpose_x(2 + x_job[0], x_job[1], TURNED_BANK)
+            take_squares(walk[k])
+            if k in (1, 2):
+                regroup_w_in(k + 1)
+            if k == 3:
+                regroup_w_out(0)
+            if k >= FIRST_ADD:
+                add_two_squares(walk[k])
+            if k == 0:
                 for m in range(COMPONENTS):
                     quantise_x(1, m)
-            if u in X_AT:
-                quantise_x(*X_AT[u])
-            if u >= 1:
-                add_squares(*walk[u - 1], bank[SUM_1[u % len(SUM_1)]])
-            for g in W_IN_AT.get(u, ()):
-                quantise_weight(w_in_codes, w_in_scales, "w_in", g)
-            for g in W_OUT_1.get(u, ()):
-                quantise_weight(w_out_codes, w_out_scales, "w_out", g)
-            if u >= 2:
-                take_inverse_norm(*walk[u - 2])
-                take_norm(*walk[u - 2])
+            if 0 <= x_job[0] < 2:
+                quantise_x(2 + x_job[0], x_job[1])
+            if k >= 1:
+                add_squares(walk[k - 1], EARLY_SUM_BANKS[k % len(EARLY_SUM_BANKS)])
+            if k in (1, 2):
+                quantise_w_in(k + 1)
+            if k == 4:
+                quantise_w_out(0)
+            if k >= 2:
+                take_root(walk[k - 2])
+                take_norm(walk[k - 2])
+        vector_cols = psum.tile([P, P], BF16, tag=bank(TURNED_BANK))
+        nc.tensor.transpose(vector_cols[:], vector_rows[:], identity[:])
+        gain_bias = keep.tile([P, 2 * F_TILES], F32)
+        nc.vector.tensor_copy(out=gain_bias[:], in_=vector_cols[:, 0 : 2 * F_TILES])
 
-        add_squares(*walk[N - 1], bank[SUM_1[N % len(SUM_1)]])
-        for m in range(GAP_SQUARES):
-            take_square(*units[N], m)
-        take_inverse_norm(*walk[N - 2])
-        for g in W_GAP0:
-            regroup_weight(w_out_raw, "w_out", g)
-        take_norm(*walk[N - 2])
-        for g in W_GAP0:
-            quantise_weight(w_out_codes, w_out_scales, "w_out", g)
-        for m in ORDER:
-            hidden_by_channel(*units[0], m, bank[CHANNEL[m]], GAP_WARM if m == ORDER[-1] else 0)
-        take_inverse_norm(*walk[N - 1])
-        for g in W_OUT_GAP:
-            regroup_weight(w_out_raw, "w_out", g)
-            quantise_weight(w_out_codes, w_out_scales, "w_out", g)
-        take_norm(*walk[N - 1])
-        copy_hidden(*units[0])
-        take_gelu(*units[0])
-        take_gelu(*units[1])
-        for g in W_OUT_GAP2:
-            regroup_weight(w_out_raw, "w_out", g)
-            quantise_weight(w_out_codes, w_out_scales, "w_out", g)
-        take_gate(*units[0])
+        add_squares(walk[EARLY - 1], EARLY_SUM_BANKS[EARLY % len(EARLY_SUM_BANKS)])
+        take_squares(EARLY)
+        take_root(walk[EARLY - 2])
+        regroup_w_out(1)
+        take_norm(walk[EARLY - 2])
+        quantise_w_out(1)
+        for m in component_order:
+            hidden_by_channel(0, m, CHANNEL_BANKS[m], WARM_CHANGE if m == component_order[-1] else 0)
+        take_root(walk[EARLY - 1])
+        take_norm(walk[EARLY - 1])
+        copy_hidden(0)
+        take_gelu(0)
+        take_gelu(1)
+        regroup_w_out(2)
+        quantise_w_out(2)
+        take_gate(0)
 
+        pieces = [(tt, piece) for tt in range(TOKEN_TILES) for piece in range(D_PIECES)]
         done = 0
-        for a in range(N):
-            if T_AT.get(a) is not None:
-                add_squares(*units[T_AT[a]], bank[SUM_2[T_AT[a]]])
-            for u in GELUS.get(a, ()):
-                take_gelu(*units[u])
-            late = ROOT_AT.get(a, ())
-            if SQ_AT.get(a) is not None and a not in ROOT_FIRST:
+        for a in range(EARLY):
+            if a in SUMS_AT:
+                add_squares(SUMS_AT[a], SUM_BANKS[SUMS_AT[a] % 2])
+            if 2 * a + 2 < EARLY:
+                take_gelu(2 * a + 2)
+                take_gelu(2 * a + 3)
+            roots = ROOTS_AT.get(a, ())
+            if a in SQUARES_AT and len(roots) < 2:
+                take_squares(SQUARES_AT[a])
+            for u in roots:
+                take_root(u)
+            if a in SQUARES_AT and len(roots) == 2:
+                take_squares(SQUARES_AT[a])
+            for m in component_order:
+                multiply_by_gate(a, m)
+                warm = 1 if a in WARM_STEPS and m == component_order[-1] else 0
+                hidden_by_channel(a + 1, m, CHANNEL_BANKS[m], warm)
+            if a in HIDDEN_AT:
                 for m in range(COMPONENTS):
-                    take_square(*units[SQ_AT[a]], m)
-            for u in late:
-                take_inverse_norm(*units[u])
-            if a in ROOT_FIRST:
-                for m in range(COMPONENTS):
-                    take_square(*units[SQ_AT[a]], m)
-            if a in ADD_FIRST:
-                add_two_squares(*units[SQ_AT[a]])
-            for m in ORDER:
-                multiply_by_gate(*units[a], m)
-                hidden_by_channel(*units[a + 1], m, bank[CHANNEL[m]], WARM.get(a, 0) if m == ORDER[-1] else 0)
-            if MM_AT.get(a) is not None:
-                for m in range(COMPONENTS):
-                    hidden_by_token(*units[MM_AT[a]], m, bank[TOKEN_2[m]])
-            copy_hidden(*units[a + 1])
-            for finished in list(accumulated):
-                store(*finished)
-            for u in LATE_GELUS.get(a, ()):
-                take_gelu(*units[u])
-            for g in W_R_2.get(a, ()):
-                regroup_weight(w_out_raw, "w_out", g)
-            if a + 1 < N:
-                take_gate(*units[a + 1])
-            for g in W_R_2.get(a, ()):
-                quantise_weight(w_out_codes, w_out_scales, "w_out", g)
-            if a in ADD_LAST:
-                add_two_squares(*units[SQ_AT[a]])
+                    hidden_by_token(HIDDEN_AT[a], m, TOKEN_BANKS[m])
+            if a + 1 not in WITHOUT_GPSIMD:
+                copy_hidden(a + 1)
+            store_waiting()
+            if 15 in roots:
+                take_gelu(EARLY)
+                take_gelu(EARLY + 1)
+            if a == 1:
+                regroup_w_out(3)
+            if a + 1 < EARLY:
+                take_gate(a + 1)
+            if a == 1:
+                quantise_w_out(3)
             if a >= 1:
-                quantise_g(*units[a - 1])
-            for u in late:
-                take_norm(*units[u])
-            for i in range(PIECES_2.get(a, 0)):
-                second_matmul(*pieces[done], bank[OUT_BANK[a][i]])
-                done = done + 1
-        take_gate(*units[N])
+                quantise_g(a - 1)
+            for u in roots:
+                take_norm(u)
+            for tt, piece in pieces[done : done + PIECES_AT.get(a, 0)]:
+                waiting.append((tt, piece, second_matmul(tt, piece, (TOKEN_BANKS + SUM_BANKS)[piece], range(GROUPS))))
+            done = done + PIECES_AT.get(a, 0)
+        take_gate(EARLY)
+
+        for a in range(EARLY, UNITS):
+            store_waiting()
+            if a + 1 < UNITS:
+                for m in component_order:
+                    hidden_by_channel(a + 1, m, (CHANNEL_BANKS, TOKEN_BANKS)[(a + 1 - EARLY) % 2][m])
+                if a + 1 not in WITHOUT_GPSIMD:
+                    copy_hidden(a + 1)
+            if a == UNITS - 1:
+                quantise_g(a - 1)
+            for m in component_order:
+                multiply_by_gate(a, m)
+            if a + 2 < UNITS:
+                take_gelu(a + 2)
+            if a + 1 < UNITS:
+                take_gate(a + 1)
+                quantise_g(a - 1)
+            for tt, piece in pieces[done : done + PIECES_AT[a]]:
+                waiting.append((tt, piece, second_matmul(tt, piece, SUM_BANKS[piece % 2], range(GROUPS))))
+            done = done + PIECES_AT[a]
+        store_waiting()
+        quantise_g(UNITS - 1)
 
         last_tile = TOKEN_TILES - 1
-        for a in range(N, UNITS):
-            for finished in list(accumulated):
-                store(*finished)
-            if a + 1 < UNITS:
-                for m in ORDER:
-                    hidden_by_channel(*units[a + 1], m, bank[CHANNEL[m] if (a + 1 - N) % 2 == 0 else TOKEN_2[m]])
-                if a + 2 < UNITS:
-                    copy_hidden(*units[a + 1])
-            if a == UNITS - 1:
-                quantise_g(*units[a - 1])
-            for m in ORDER:
-                multiply_by_gate(*units[a], m)
-            if a + 2 < UNITS:
-                take_gelu(*units[a + 2])
-            if a + 1 < UNITS:
-                take_gate(*units[a + 1])
-            if a < UNITS - 1:
-                quantise_g(*units[a - 1])
-            for piece in pieces[done : done + PIECES_3[a]]:
-                second_matmul(*piece, bank[SUM[done % 2]])
-                done = done + 1
-        for finished in list(accumulated):
-            store(*finished)
-        quantise_g(*units[UNITS - 1])
-        partial = []
-        final_banks = CHANNEL + TOKEN_2 + SUM
-        for piece in range(D_PIECES):
-            second_matmul(last_tile, piece, bank[FINAL[piece]], range(GROUPS - 1))
-            partial.append(stage.tile([P, P, COMPONENTS], F32, name="partial%d" % piece, bufs=1))
-            nc.scalar.copy(out=partial[piece][:], in_=accumulated.pop((last_tile, piece))[:].rearrange("p m d -> p d m"))
-        for piece in range(D_PIECES):
-            second_matmul(last_tile, piece, bank[FINAL[D_PIECES + piece]], range(GROUPS - 1, GROUPS))
-            store(last_tile, piece, partial[piece])
+        partials = []
+        for piece in range(MERGED_PIECES):
+            acc = second_matmul(last_tile, piece, TOKEN_BANKS[piece], range(GROUPS - 1))
+            partials.append(stage.tile([P, P, COMPONENTS], F32, name="partial%d" % piece, bufs=1))
+            nc.scalar.copy(out=partials[piece][:], in_=acc)
+        for piece in range(MERGED_PIECES):
+            acc = second_matmul(last_tile, piece, (SUM_BANKS[1], CHANNEL_BANKS[0])[piece], range(GROUPS - 1, GROUPS))
+            store(last_tile, piece, acc, partials[piece])
+        for piece in range(MERGED_PIECES, D_PIECES):
+            store(last_tile, piece, second_matmul(last_tile, piece, CHANNEL_BANKS[piece - 1], range(GROUPS)))

from contextlib import ExitStack

import concourse.mybir as mybir
from concourse.masks import make_identity

F32 = mybir.dt.float32
BF16 = mybir.dt.bfloat16
U32 = mybir.dt.uint32
U8 = mybir.dt.uint8
FP8X4 = mybir.dt.float8_e4m3fn_x4
ACT = mybir.ActivationFunctionType
ALU = mybir.AluOpType

P = 128
PACK = 4
K_PASS = P * PACK
TOKEN_TILES = 4
COMPONENTS = 3
D = 512
F = 2048
GROUPS = F // K_PASS
F_TILES = F // P
D_PIECES = D // P
UNITS = TOKEN_TILES * GROUPS
RUN = 4
RUNS = P // RUN
MAX_INVERSE_NORM = 1e12
FLOPS = 2 * 2 * TOKEN_TILES * P * COMPONENTS * D * F

EARLY = 10
EARLY_WALK = (0, 1, 4, 5, 2, 6, 3, 7, 8, 9)
FIRST_ADD = 4
SCALAR_COLUMNS = 256

HIDDEN_AT = {0: 11, 3: 12, 4: 13, 5: 14, 6: 15}
SQUARES_AT = {2: 11, 4: 12, 5: 13, 6: 14, 7: 15}
SUMS_AT = {1: 10, 3: 11, 5: 12, 6: 13, 7: 14, 8: 15}
ROOTS_AT = {4: (10, 11), 5: (12,), 6: (13,), 7: (14,), 8: (15,)}
PIECES_AT = {8: 2, 9: 2, 10: 1, 11: 1, 12: 2, 13: 2, 14: 1, 15: 1}
GPSIMD_RUN = 3
WITHOUT_GPSIMD = (4, UNITS - 1)

WARM_HEAD = (5, 3)
WARM_CHANGE = 12
WARM_STEPS = (1, 2, 3)

CHANNEL_BANKS = (0, 1, 2)
TOKEN_BANKS = (3, 4, 5)
SUM_BANKS = (6, 7)
EARLY_TOKEN_BANKS = (3, 4, 5, 0)
EARLY_SUM_BANKS = (6, 7, 1)
TURNED_BANK = 2
X1_BANKS = (2, 6, 7)
MERGED_PIECES = 2


def tile_feedforwardse3_pa_kernel(tc, x, w_in, scale, bias, w_out, out):
    nc = tc.nc
    x_rows = x.rearrange("b n d m -> b n (d m)")
    out_rows = out.rearrange("b n d m -> b n (d m)")
    w_in_pieces = w_in.rearrange("(j p) (g f) -> g p j f", p=P, g=GROUPS)
    w_out_pieces = w_out.rearrange("(g j p) d -> g p j d", j=PACK, p=P)

    with ExitStack() as ctx:
        keep = ctx.enter_context(tc.tile_pool(name="keep", bufs=1))
        stage = ctx.enter_context(tc.tile_pool(name="stage", bufs=2))
        psum = ctx.enter_context(tc.psum_pool(name="psum", bufs=1))
        ctx.enter_context(tc.manual_schedule())

        def bank(index):
            return "bank%d" % index

        identity = keep.tile([P, P], BF16)
        vector_rows = keep.tile([P, P], BF16)
        one = keep.tile([P, 1], F32)
        zeros = keep.tile([P, K_PASS], BF16)
        nc.vector.memset(vector_rows[:], 0.0)
        nc.vector.memset(zeros[:], 0.0)
        nc.vector.memset(one[:], 1.0)
        x_raw = {}
        w_in_raw = {}
        w_out_raw = {}

        def load_x(tt):
            x_raw[tt] = keep.tile([P, D * COMPONENTS], BF16, name="x_raw%d" % tt)
            nc.sync.dma_start(out=x_raw[tt][:], in_=x_rows[tt])

        def load_weight(raw, pieces, g, name):
            raw[g] = keep.tile([P, PACK, K_PASS], BF16, name="%s%d" % (name, g))
            nc.sync.dma_start(out=raw[g][:], in_=pieces[g])

        load_x(0)
        load_weight(w_in_raw, w_in_pieces, 0, "w_in_raw")
        load_weight(w_in_raw, w_in_pieces, 1, "w_in_raw")
        load_x(1)
        load_weight(w_in_raw, w_in_pieces, 2, "w_in_raw")
        load_weight(w_in_raw, w_in_pieces, 3, "w_in_raw")
        load_x(2)
        load_x(3)
        nc.sync.dma_start(out=vector_rows[0:F_TILES, :], in_=scale.rearrange("a b (r c) -> (a b r) c", c=P))
        nc.sync.dma_start(out=vector_rows[F_TILES : 2 * F_TILES, :], in_=bias.rearrange("a b (r c) -> (a b r) c", c=P))
        for g in range(GROUPS):
            load_weight(w_out_raw, w_out_pieces, g, "w_out_raw")

        make_identity(nc, identity[:])
        identity_f32 = keep.tile([P, P], F32)
        make_identity(nc, identity_f32[:])
        one_out = keep.tile([P, 1], F32)
        nc.scalar.activation(out=one_out[:], in_=one[:], func=ACT.Abs_reciprocal_sqrt)

        w_grouped = {}
        w_in_codes = {}
        w_in_scales = {}
        w_out_codes = {}
        w_out_scales = {}

        def regroup_columns(copy, raw, name, g, first, last):
            copy(
                out=w_grouped[name, g][:, first:last].rearrange("p (c i) j -> p c j i", i=4),
                in_=raw[g][:, :, first:last].rearrange("p j (c i) -> p c j i", i=4),
            )

        def regroup_weight(raw, name, g, scalar_columns=0):
            w_grouped[name, g] = stage.tile([P, K_PASS, PACK], BF16, align_bytes=64, name="w_grouped")
            if scalar_columns > 0:
                regroup_columns(nc.scalar.copy, raw, name, g, 0, scalar_columns)
            regroup_columns(nc.vector.tensor_copy, raw, name, g, scalar_columns, K_PASS)

        def quantise_weight(codes, scales, name, g):
            codes[g] = keep.tile([P, K_PASS], U32, align_bytes=64, name="%s_codes%d" % (name, g))
            scales[g] = keep.tile([P, K_PASS], U8, align_bytes=64, name="%s_scales%d" % (name, g))
            nc.vector.quantize_mx(
                out=codes[g][:].bitcast(FP8X4), scales=scales[g][:], in_=w_grouped[name, g][:].rearrange("p w j -> p (w j)")
            )

        def regroup_w_in(g, scalar_columns=0):
            regroup_weight(w_in_raw, "w_in", g, scalar_columns)

        def quantise_w_in(g):
            quantise_weight(w_in_codes, w_in_scales, "w_in", g)

        def regroup_w_out(g):
            regroup_weight(w_out_raw, "w_out", g)

        def quantise_w_out(g):
            quantise_weight(w_out_codes, w_out_scales, "w_out", g)

        x_grouped = {}
        x_codes = {}
        x_scales = {}

        def transpose_x(tt, m, bank_index):
            x_dm = x_raw[tt][:].rearrange("p (d m) -> p d m", m=COMPONENTS)
            x_grouped[tt, m] = stage.tile([P, P, PACK], BF16, align_bytes=64, name="x_grouped%d" % m)
            x_t = psum.tile([P, PACK, P], BF16, tag=bank(bank_index))
            for j in range(PACK):
                nc.tensor.transpose(x_t[:, j, :], x_dm[:, j * P : (j + 1) * P, m], identity[:])
            copy = nc.scalar.copy if tt == 0 else nc.vector.tensor_copy
            copy(
                out=x_grouped[tt, m][:].rearrange("p (c i) j -> p c i j", i=RUN),
                in_=x_t[:].rearrange("p j (i c) -> p c i j", i=RUN),
            )

        def quantise_x(tt, m):
            if m == 0:
                x_codes[tt] = keep.tile([P, COMPONENTS, P], U32, align_bytes=64, name="x_codes%d" % tt)
                x_scales[tt] = keep.tile([P, COMPONENTS, P], U8, align_bytes=64, name="x_scales%d" % tt)
            nc.vector.quantize_mx(
                out=x_codes[tt][:, m, :].bitcast(FP8X4),
                scales=x_scales[tt][:, m, :],
                in_=x_grouped[tt, m][:].rearrange("p t j -> p (t j)"),
            )

        token_hidden = {}
        squares = {}
        two_squares = {}
        sum_squares = {}
        inverse_norm = {}
        norm = {}

        def hidden_by_token(u, m, bank_index):
            tt, g = u // GROUPS, u % GROUPS
            token_hidden[u, m] = psum.tile([P, K_PASS], F32, tag=bank(bank_index), name="token_hidden")
            nc.tensor.matmul_mx(
                out=token_hidden[u, m][:],
                lhsT=x_codes[tt][:, m, :].bitcast(FP8X4),
                lhsT_scale=x_scales[tt][:, m, :],
                rhs=w_in_codes[g][:].bitcast(FP8X4),
                rhs_scale=w_in_scales[g][:],
                start=True,
                stop=True,
            )

        def take_squares(u):
            for m in range(COMPONENTS):
                squares[u, m] = stage.tile([P, K_PASS], F32, name="square%d" % m, bufs=3)
                nc.scalar.activation(out=squares[u, m][:], in_=token_hidden[u, m][:], func=ACT.Square)

        def add_two_squares(u):
            two_squares[u] = stage.tile([P, K_PASS], F32, name="two_squares", bufs=3)
            nc.vector.tensor_tensor(out=two_squares[u][:], in0=squares[u, 0][:], in1=squares[u, 1][:], op=ALU.add)

        def add_squares(u, bank_index):
            sum_squares[u] = psum.tile([P, RUNS, PACK, RUN], F32, tag=bank(bank_index), name="sum_squares")
            if u in two_squares:
                addends = (two_squares[u], squares[u, 2])
            else:
                addends = tuple(squares[u, m] for m in range(COMPONENTS))
            for j in range(PACK):
                for k in range(len(addends)):
                    nc.tensor.matmul(
                        sum_squares[u][:, :, j, :],
                        lhsT=addends[k][:, j * P : (j + 1) * P],
                        rhs=identity_f32[:],
                        is_transpose=True,
                        start=(k == 0),
                        stop=(k == len(addends) - 1),
                    )

        def take_root(u):
            inverse_norm[u] = stage.tile([P, RUNS, PACK, RUN], F32, name="inverse_norm", bufs=14)
            nc.scalar.activation(out=inverse_norm[u][:], in_=sum_squares[u][:], func=ACT.Abs_reciprocal_sqrt)

        def take_norm(u):
            norm[u] = stage.tile([P, RUNS, PACK, RUN], F32, name="norm", bufs=12)
            nc.vector.scalar_tensor_tensor(
                out=norm[u][:],
                in0=inverse_norm[u][:],
                scalar=MAX_INVERSE_NORM,
                in1=sum_squares[u][:],
                op0=ALU.min,
                op1=ALU.mult,
            )

        gelu = {}
        gate = {}
        channel_hidden = {}
        h_copy = {}
        g_grouped = {}
        g_codes = {}
        g_scales = {}
        component_order = (0, 2, 1)

        def take_gelu(u):
            gelu[u] = stage.tile([P, RUNS, PACK, RUN], F32, name="gelu", bufs=8)
            for j in range(PACK):
                ft = u % GROUPS * PACK + j
                nc.scalar.activation(
                    out=gelu[u][:, :, j, :],
                    in_=norm[u][:, :, j, :],
                    func=ACT.Gelu,
                    bias=gain_bias[:, F_TILES + ft : F_TILES + ft + 1],
                    scale=gain_bias[:, ft : ft + 1],
                )

        def take_gate(u):
            gate[u] = stage.tile([P, RUN, RUNS, PACK], F32, name="gate", bufs=3)
            nc.vector.scalar_tensor_tensor(
                out=gate[u][:].rearrange("p i c j -> p (c j) i"),
                in0=inverse_norm[u][:].rearrange("p c j i -> p (c j) i"),
                scalar=MAX_INVERSE_NORM,
                in1=gelu[u][:].rearrange("p c j i -> p (c j) i"),
                op0=ALU.min,
                op1=ALU.mult,
            )

        def hidden_by_channel(u, m, bank_index, warm=0):
            tt, g = u // GROUPS, u % GROUPS
            h = psum.tile([P, PACK, P], F32, tag=bank(bank_index))
            for again in range(warm):
                nc.tensor.matmul(
                    h[:].rearrange("p j t -> p (j t)"), lhsT=identity[:], rhs=x_raw[0][:, 0:K_PASS], start=True, stop=True
                )
            for j in range(PACK):
                cols = slice(j * P, (j + 1) * P)
                nc.tensor.matmul_mx(
                    out=h[:, j, :],
                    lhsT=w_in_codes[g][:, cols].bitcast(FP8X4),
                    lhsT_scale=w_in_scales[g][:, cols],
                    rhs=x_codes[tt][:, m, :].bitcast(FP8X4),
                    rhs_scale=x_scales[tt][:, m, :],
                    start=True,
                    stop=True,
                )
            channel_hidden[u, m] = h[:].rearrange("p j (c i) -> p i c j", i=RUN)

        def copy_hidden(u):
            h_copy[u] = stage.tile([P, GPSIMD_RUN, RUNS, PACK], F32, name="h_copy")
            nc.scalar.copy(out=h_copy[u][:], in_=channel_hidden[u, COMPONENTS - 1][:, 0:GPSIMD_RUN])

        def multiply_by_gate(u, m):
            g_grouped[u, m] = stage.tile([P, RUN, RUNS, PACK], BF16, align_bytes=64, name="g_grouped%d" % m, bufs=2)
            first = 0
            if m == COMPONENTS - 1 and u in h_copy:
                first = GPSIMD_RUN
                nc.gpsimd.tensor_tensor(
                    out=g_grouped[u, m][:, 0:first], in0=h_copy[u][:], in1=gate[u][:, 0:first], op=ALU.mult
                )
            nc.vector.tensor_tensor(
                out=g_grouped[u, m][:, first:], in0=channel_hidden[u, m][:, first:], in1=gate[u][:, first:], op=ALU.mult
            )

        def quantise_g(u):
            tt, g = u // GROUPS, u % GROUPS
            if g == 0:
                g_codes[tt] = stage.tile([P, GROUPS, COMPONENTS, P], U32, align_bytes=64, name="g_codes", bufs=3)
                g_scales[tt] = stage.tile([P, GROUPS, COMPONENTS, P], U8, align_bytes=64, name="g_scales", bufs=3)
            for m in range(COMPONENTS):
                nc.vector.quantize_mx(
                    out=g_codes[tt][:, g, m, :].bitcast(FP8X4),
                    scales=g_scales[tt][:, g, m, :],
                    in_=g_grouped[u, m][:].rearrange("p i c j -> p (i c j)"),
                )

        waiting = []

        def second_matmul(tt, piece, bank_index, groups):
            acc = psum.tile([P, COMPONENTS, P], F32, tag=bank(bank_index), name="acc")
            cols = slice(piece * P, (piece + 1) * P)
            for m in range(COMPONENTS):
                for g in groups:
                    nc.tensor.matmul_mx(
                        out=acc[:, m, :],
                        lhsT=g_codes[tt][:, g, m, :].bitcast(FP8X4),
                        lhsT_scale=g_scales[tt][:, g, m, :],
                        rhs=w_out_codes[g][:, cols].bitcast(FP8X4),
                        rhs_scale=w_out_scales[g][:, cols],
                        start=(g == groups[0]),
                        stop=(g == groups[-1]),
                    )
            return acc[:].rearrange("p m d -> p d m")

        def store(tt, piece, acc, partial=None):
            out_piece = stage.tile([P, P, COMPONENTS], F32, bufs=4)
            if partial is None:
                nc.scalar.copy(out=out_piece[:], in_=acc)
            else:
                nc.vector.tensor_tensor(out=out_piece[:], in0=acc, in1=partial[:], op=ALU.add)
            nc.sync.dma_start(
                out=out_rows[tt][:, piece * P * COMPONENTS : (piece + 1) * P * COMPONENTS],
                in_=out_piece[:].rearrange("p d m -> p (d m)"),
            )

        def store_waiting():
            for tt, piece, acc in waiting:
                store(tt, piece, acc)
            waiting.clear()

        def keep_warm(bank_index, count):
            idle = psum.tile([P, K_PASS], F32, tag=bank(bank_index), name="idle")
            for again in range(count):
                nc.tensor.matmul(idle[:], lhsT=zeros[:, 0:P], rhs=zeros[:], start=True, stop=True)

        keep_warm(TOKEN_BANKS[0], WARM_HEAD[0])
        for m in range(COMPONENTS):
            transpose_x(0, m, CHANNEL_BANKS[m])
        keep_warm(TOKEN_BANKS[0], WARM_HEAD[1])
        regroup_w_in(0)
        quantise_x(0, 0)
        quantise_w_in(0)
        quantise_x(0, 1)
        quantise_x(0, 2)
        regroup_w_in(1, SCALAR_COLUMNS)
        quantise_w_in(1)

        token_banks = [
            EARLY_TOKEN_BANKS[(COMPONENTS * k + m) % len(EARLY_TOKEN_BANKS)] for k in range(EARLY) for m in range(COMPONENTS)
        ] + list(TOKEN_BANKS)
        walk = list(EARLY_WALK) + [EARLY]
        for m in range(COMPONENTS):
            hidden_by_token(walk[0], m, token_banks[m])
        for m in range(COMPONENTS):
            transpose_x(1, m, X1_BANKS[m])
        for k in range(EARLY):
            for m in range(COMPONENTS):
                hidden_by_token(walk[k + 1], m, token_banks[COMPONENTS * (k + 1) + m])
            x_job = divmod(k - 3, COMPONENTS)
            if 0 <= x_job[0] < 2:
                transpose_x(2 + x_job[0], x_job[1], TURNED_BANK)
            take_squares(walk[k])
            if k in (1, 2):
                regroup_w_in(k + 1)
            if k == 3:
                regroup_w_out(0)
            if k >= FIRST_ADD:
                add_two_squares(walk[k])
            if k == 0:
                for m in range(COMPONENTS):
                    quantise_x(1, m)
            if 0 <= x_job[0] < 2:
                quantise_x(2 + x_job[0], x_job[1])
            if k >= 1:
                add_squares(walk[k - 1], EARLY_SUM_BANKS[k % len(EARLY_SUM_BANKS)])
            if k in (1, 2):
                quantise_w_in(k + 1)
            if k == 4:
                quantise_w_out(0)
            if k >= 2:
                take_root(walk[k - 2])
                take_norm(walk[k - 2])
        vector_cols = psum.tile([P, P], BF16, tag=bank(TURNED_BANK))
        nc.tensor.transpose(vector_cols[:], vector_rows[:], identity[:])
        gain_bias = keep.tile([P, 2 * F_TILES], F32)
        nc.vector.tensor_copy(out=gain_bias[:], in_=vector_cols[:, 0 : 2 * F_TILES])

        add_squares(walk[EARLY - 1], EARLY_SUM_BANKS[EARLY % len(EARLY_SUM_BANKS)])
        take_squares(EARLY)
        take_root(walk[EARLY - 2])
        regroup_w_out(1)
        take_norm(walk[EARLY - 2])
        quantise_w_out(1)
        for m in component_order:
            hidden_by_channel(0, m, CHANNEL_BANKS[m], WARM_CHANGE if m == component_order[-1] else 0)
        take_root(walk[EARLY - 1])
        take_norm(walk[EARLY - 1])
        copy_hidden(0)
        take_gelu(0)
        take_gelu(1)
        regroup_w_out(2)
        quantise_w_out(2)
        take_gate(0)

        pieces = [(tt, piece) for tt in range(TOKEN_TILES) for piece in range(D_PIECES)]
        done = 0
        for a in range(EARLY):
            if a in SUMS_AT:
                add_squares(SUMS_AT[a], SUM_BANKS[SUMS_AT[a] % 2])
            if 2 * a + 2 < EARLY:
                take_gelu(2 * a + 2)
                take_gelu(2 * a + 3)
            roots = ROOTS_AT.get(a, ())
            if a in SQUARES_AT and len(roots) < 2:
                take_squares(SQUARES_AT[a])
            for u in roots:
                take_root(u)
            if a in SQUARES_AT and len(roots) == 2:
                take_squares(SQUARES_AT[a])
            for m in component_order:
                multiply_by_gate(a, m)
                warm = 1 if a in WARM_STEPS and m == component_order[-1] else 0
                hidden_by_channel(a + 1, m, CHANNEL_BANKS[m], warm)
            if a in HIDDEN_AT:
                for m in range(COMPONENTS):
                    hidden_by_token(HIDDEN_AT[a], m, TOKEN_BANKS[m])
            if a + 1 not in WITHOUT_GPSIMD:
                copy_hidden(a + 1)
            store_waiting()
            if 15 in roots:
                take_gelu(EARLY)
                take_gelu(EARLY + 1)
            if a == 1:
                regroup_w_out(3)
            if a + 1 < EARLY:
                take_gate(a + 1)
            if a == 1:
                quantise_w_out(3)
            if a >= 1:
                quantise_g(a - 1)
            for u in roots:
                take_norm(u)
            for tt, piece in pieces[done : done + PIECES_AT.get(a, 0)]:
                waiting.append((tt, piece, second_matmul(tt, piece, (TOKEN_BANKS + SUM_BANKS)[piece], range(GROUPS))))
            done = done + PIECES_AT.get(a, 0)
        take_gate(EARLY)

        for a in range(EARLY, UNITS):
            store_waiting()
            if a + 1 < UNITS:
                for m in component_order:
                    hidden_by_channel(a + 1, m, (CHANNEL_BANKS, TOKEN_BANKS)[(a + 1 - EARLY) % 2][m])
                if a + 1 not in WITHOUT_GPSIMD:
                    copy_hidden(a + 1)
            if a == UNITS - 1:
                quantise_g(a - 1)
            for m in component_order:
                multiply_by_gate(a, m)
            if a + 2 < UNITS:
                take_gelu(a + 2)
            if a + 1 < UNITS:
                take_gate(a + 1)
                quantise_g(a - 1)
            for tt, piece in pieces[done : done + PIECES_AT[a]]:
                waiting.append((tt, piece, second_matmul(tt, piece, SUM_BANKS[piece % 2], range(GROUPS))))
            done = done + PIECES_AT[a]
        store_waiting()
        quantise_g(UNITS - 1)

        last_tile = TOKEN_TILES - 1
        partials = []
        for piece in range(MERGED_PIECES):
            acc = second_matmul(last_tile, piece, TOKEN_BANKS[piece], range(GROUPS - 1))
            partials.append(stage.tile([P, P, COMPONENTS], F32, name="partial%d" % piece, bufs=1))
            nc.scalar.copy(out=partials[piece][:], in_=acc)
        for piece in range(MERGED_PIECES):
            acc = second_matmul(last_tile, piece, (SUM_BANKS[1], CHANNEL_BANKS[0])[piece], range(GROUPS - 1, GROUPS))
            store(last_tile, piece, acc, partials[piece])
        for piece in range(MERGED_PIECES, D_PIECES):
            store(last_tile, piece, second_matmul(last_tile, piece, CHANNEL_BANKS[piece - 1], range(GROUPS)))
